import numpy as np
import ml_dtypes


def mxq(x, axis, fmt="e4m3"):
    dtype, down = {"e4m3": (ml_dtypes.float8_e4m3fn, 7), "e5m2": (ml_dtypes.float8_e5m2, 14)}[fmt]
    v = np.moveaxis(np.asarray(x, np.float32).astype(ml_dtypes.bfloat16).astype(np.float64), axis, -1)
    blocks = v.reshape(v.shape[:-1] + (-1, 32))
    amax = np.abs(blocks).max(-1, keepdims=True)
    byte = np.maximum(np.where(amax > 0, np.frexp(amax)[1] - 1 + 127, 0) - down, 1)
    scale = np.exp2(byte - 127.0)
    codes = (blocks / scale).astype(np.float32).astype(dtype).astype(np.float64)
    return np.moveaxis((codes * scale).reshape(v.shape), -1, axis)


WIDE = False


def mx_kscale(k):
    if not WIDE:
        return np.ones(k)
    levels = np.array([10, -10, 5, -5, 0])
    if k % 512:
        return np.exp2(np.random.permutation(np.resize(levels, k // 32))).repeat(32)
    a = np.empty((k // 512, 16))
    for p in range(k // 512):
        a[p, :8] = np.random.permutation(np.resize(levels, 8))
        for g in range(8):
            far = levels[np.abs(levels - a[p, g]) >= 10]
            a[p, g + 8] = far[np.random.randint(len(far))]
    return np.exp2(a.ravel()).repeat(32)


BF16 = ml_dtypes.bfloat16


def bf(x):
    return np.asarray(x, np.float32).astype(BF16)


def f64(x):
    return np.asarray(x).astype(np.float64)


B, O, A, H, Z = 256, 512, 512, 1536, 512
CLAMP = 10.0
LV_LO, LV_HI = -12.0, 2.0


def setup_inputs():
    s, t = mx_kscale(O + H), mx_kscale(H)
    return {
        "x_t": bf(np.random.standard_normal((B, O)) * s[:O]),
        "h_prev": bf(np.random.standard_normal((B, H)) * s[O:]),
        "eps": bf(np.random.standard_normal((B, Z))),
        "enc_w1": bf(np.random.standard_normal((H, O + H)) / np.sqrt(O + H) * t[:, None] / s[None, :]),
        "enc_b1": bf(np.random.standard_normal(H) * 0.1 * t),
        "enc_w2": bf(np.random.standard_normal((2 * Z, H)) * 1.4 / np.sqrt(H) / t[None, :]),
        "enc_b2": bf(np.concatenate([np.random.standard_normal(Z) * 0.1, np.random.uniform(LV_LO, LV_HI, Z)])),
        "mu_p": bf(np.random.standard_normal((B, Z)) * 0.7),
        "logvar_p": bf(np.random.standard_normal((B, Z)) * 0.7),
    }


def reference(x_t, h_prev, eps, enc_w1, enc_b1, enc_w2, enc_b2, mu_p, logvar_p):
    mu_p, logvar_p = f64(mu_p), f64(logvar_p)
    xh = np.concatenate([f64(x_t), f64(h_prev)], -1)
    hid = np.maximum((mxq(xh, 1, "e4m3") @ mxq(f64(enc_w1), 1, "e4m3").T) + f64(enc_b1), 0.0)
    stats = (mxq(hid, 1, "e4m3") @ mxq(f64(enc_w2), 1, "e4m3").T) + f64(enc_b2)
    mu_q = stats[:, :Z]
    logvar_q = np.clip(stats[:, Z:], -CLAMP, CLAMP)
    std_q = np.exp(0.5 * logvar_q)
    z_t = mu_q + f64(eps) * std_q
    var_p = np.exp(logvar_p)
    kl = 0.5 * np.sum((mu_q - mu_p) ** 2 / var_p + np.exp(logvar_q) / var_p + (logvar_p - logvar_q) - 1.0, axis=-1)
    return z_t, mu_q, logvar_q, kl

@@ -1,0 +1,346 @@
+from contextlib import ExitStack
+
+import concourse.mybir as mybir
+from concourse.masks import make_identity
+
+F32 = mybir.dt.float32
+BF16 = mybir.dt.bfloat16
+U32 = mybir.dt.uint32
+U8 = mybir.dt.uint8
+FP8X4 = mybir.dt.float8_e4m3fn_x4
+ACT = mybir.ActivationFunctionType
+ALU = mybir.AluOpType
+
+P = 128
+K_PASS = 4 * P
+PAIR = 2 * P
+
+B, O, H, Z = 256, 512, 1536, 512
+K1 = O + H
+PASSES1 = K1 // K_PASS
+PASSES2 = H // K_PASS
+W1_PAIRS = H // PAIR
+W2_PAIRS = 2 * Z // PAIR
+B_TILES = B // P
+Z_PARTS = Z // PAIR
+CLAMP = 10.0
+PREPARE_AHEAD = 2
+KL_TERMS = 3
+DEV_SQ, LV_DIFF, VAR_RATIO = 0, 1, 2
+
+FLOPS = 2 * B * K1 * H + 2 * B * H * 2 * Z
+
+
+def tile_vrnncell_pa_kernel(
+    tc, x_t, h_prev, eps, enc_w1, enc_b1, enc_w2, enc_b2, mu_p, logvar_p, out_0, out_1, out_2, out_3
+):
+    nc = tc.nc
+    with ExitStack() as ctx:
+        keep = ctx.enter_context(tc.tile_pool(name="keep", bufs=1))
+        stage = ctx.enter_context(tc.tile_pool(name="stage", bufs=6))
+        psum_t = ctx.enter_context(tc.psum_pool(name="psum_t", bufs=6))
+        psum_acc = ctx.enter_context(tc.psum_pool(name="psum_acc", bufs=2))
+        ctx.enter_context(tc.manual_schedule())
+
+        def load_rows(rows, width, name):
+            raw = keep.tile([P, 2 * width], BF16, name=name)
+            nc.sync.dma_start(out=raw[:].rearrange("p (a k) -> p a k", a=2), in_=rows)
+            return raw[:].bitcast(F32).rearrange("p (a w) -> p a w", a=2)
+
+        def load_pair(rows, width, name):
+            return load_rows(rows.rearrange("(p a) k -> p a k", a=2), width, name)
+
+        def load_w1_pair(c):
+            quad = enc_w1[c // 2 * K_PASS : (c // 2 + 1) * K_PASS, :].rearrange("(p t) k -> p t k", t=4)
+            return load_rows(quad[:, c % 2 * 2 : c % 2 * 2 + 2, :], K1, "w1_raw%d" % c)
+
+        x_words = load_pair(x_t, O, "x_raw")
+        h_words = load_pair(h_prev, H, "h_raw")
+        w1_words = [load_w1_pair(c) for c in range(W1_PAIRS)]
+
+        def load_prior(src, name):
+            prior = keep.tile([P, B_TILES, Z], BF16, name=name)
+            nc.sync.dma_start(out=prior[:], in_=src.rearrange("(t p) z -> p t z", p=P))
+            return prior
+
+        lvp_sb = load_prior(logvar_p, "lvp_sb")
+        mup_sb = load_prior(mu_p, "mup_sb")
+        eps_sb = load_prior(eps, "eps_sb")
+        w2_words = [
+            load_pair(enc_w2[q * PAIR : (q + 1) * PAIR, :], H, "w2_raw%d" % q) for q in range(W2_PAIRS)
+        ]
+
+        ident = keep.tile([P, P], F32)
+        make_identity(nc, ident[:])
+        ones = keep.tile([P, P], BF16)
+        nc.gpsimd.memset(ones[:], 1.0)
+        b1_rows = keep.tile([P, PAIR], F32)
+        nc.gpsimd.memset(b1_rows[:], 0.0)
+        nc.scalar.dma_start(
+            out=b1_rows[:].bitcast(BF16)[0:PASSES2, :], in_=enc_b1.rearrange("(g w) -> g w", g=PASSES2)
+        )
+        b2_row = keep.tile([P, 2 * Z], BF16)
+        nc.gpsimd.memset(b2_row[:], 0.0)
+        nc.scalar.dma_start(out=b2_row[0:1, :], in_=enc_b2.rearrange("(o n) -> o n", o=1))
+        kl_sums = keep.tile([P, KL_TERMS * Z_PARTS, P], F32)
+        nc.gpsimd.memset(kl_sums[:], 0.0)
+
+        warm = keep.tile([P, 1], F32)
+        nc.vector.memset(warm[:], 0.0)
+        nc.scalar.activation(out=warm[:], in_=warm[:], func=ACT.Exp)
+
+        x_codes = keep.tile([P, PASSES1, B], U32, align_bytes=64)
+        x_scales = keep.tile([P, PASSES1, B], U8, align_bytes=64)
+        w1_codes = keep.tile([P, W1_PAIRS, PASSES1, PAIR], U32, align_bytes=64)
+        w1_scales = keep.tile([P, W1_PAIRS, PASSES1, PAIR], U8, align_bytes=64)
+        hid_codes = keep.tile([P, PASSES2, B], U32, align_bytes=64)
+        hid_scales = keep.tile([P, PASSES2, B], U8, align_bytes=64)
+        w2_codes = keep.tile([P, W2_PAIRS, PASSES2, PAIR], U32, align_bytes=64)
+        w2_scales = keep.tile([P, W2_PAIRS, PASSES2, PAIR], U8, align_bytes=64)
+
+        def transpose_pass(words, g):
+            bank = psum_t.tile([P, 4 * P], F32)
+            for a in range(2):
+                for u in range(2):
+                    nc.tensor.transpose(
+                        out=bank[:, (2 * a + u) * P : (2 * a + u + 1) * P],
+                        in_=words[:, a, 2 * g * P + u : 2 * (g + 1) * P : 2],
+                        identity=ident[:],
+                    )
+            return bank
+
+        def group_rows_in_order(copy, bank):
+            grouped = stage.tile([P, 4 * PAIR], BF16, align_bytes=64)
+            copy(
+                out=grouped[:].bitcast(F32).rearrange("p (r a u) -> p r a u", a=2, u=2),
+                in_=bank[:].rearrange("p (a u r) -> p r a u", a=2, u=2),
+            )
+            return grouped
+
+        def group_rows_even_odd(copy, bank):
+            grouped = stage.tile([P, 4 * PAIR], BF16, align_bytes=64)
+            copy(
+                out=grouped[:].bitcast(F32).rearrange("p (a r u) -> p a r u", a=2, u=2),
+                in_=bank[:].rearrange("p (a u r) -> p a r u", a=2, u=2),
+            )
+            return grouped
+
+        def quantise(grouped, codes, scales):
+            nc.vector.quantize_mx(out=codes.bitcast(FP8X4), scales=scales, in_=grouped[:])
+
+        x_banks = [transpose_pass(x_words, 0)] + [transpose_pass(h_words, g) for g in range(PASSES1 - 1)]
+        x_grouped = [
+            group_rows_in_order(nc.vector.tensor_copy if g % 2 == 0 else nc.scalar.copy, x_banks[g])
+            for g in range(PASSES1)
+        ]
+        for g in range(PASSES1):
+            quantise(x_grouped[g], x_codes[:, g, :], x_scales[:, g, :])
+
+        b1_bank = psum_t.tile([P, 4 * P], F32, tag="bank")
+        for h in range(2):
+            nc.tensor.transpose(out=b1_bank[:, h * P : (h + 1) * P], in_=b1_rows[:, h::2], identity=ident[:])
+        b1_cols = keep.tile([P, PASSES2, 4], F32)
+        for h in range(2):
+            nc.vector.tensor_copy(
+                out=b1_cols[:, :, 2 * h : 2 * h + 2],
+                in_=b1_bank[:].bitcast(BF16)[:, h * PAIR : h * PAIR + 2 * PASSES2].rearrange("p (g e) -> p g e", e=2),
+            )
+
+        b2_all = keep.tile([P, 2 * Z], F32)
+        for half in range(2):
+            b2_bank = psum_acc.tile([P, Z], F32, tag="acc")
+            nc.tensor.matmul(
+                out=b2_bank[:], lhsT=ones[:], rhs=b2_row[:, half * Z : (half + 1) * Z], start=True, stop=True
+            )
+            nc.vector.tensor_copy(out=b2_all[:, half * Z : (half + 1) * Z], in_=b2_bank[:])
+
+        hid_rows = keep.tile([P, 2 * W1_PAIRS, B], BF16)
+
+        def prepare_w1(c):
+            banks = [transpose_pass(w1_words[c], g) for g in range(PASSES1)]
+            grouped = [
+                group_rows_even_odd(nc.vector.tensor_copy if g == PASSES1 - 1 else nc.scalar.copy, banks[g])
+                for g in range(PASSES1)
+            ]
+            for g in range(PASSES1):
+                quantise(grouped[g], w1_codes[:, c, g, :], w1_scales[:, c, g, :])
+
+        def layer1(c):
+            hid_acc = psum_acc.tile([P, 2, B], F32, tag="acc")
+            for e in range(2):
+                for g in range(PASSES1):
+                    nc.tensor.matmul_mx(
+                        out=hid_acc[:, e, :],
+                        lhsT=w1_codes[:, c, g, e * P : (e + 1) * P].bitcast(FP8X4),
+                        lhsT_scale=w1_scales[:, c, g, e * P : (e + 1) * P],
+                        rhs=x_codes[:, g, :].bitcast(FP8X4),
+                        rhs_scale=x_scales[:, g, :],
+                        start=(g == 0),
+                        stop=(g == PASSES1 - 1),
+                    )
+            for e in range(2):
+                nc.scalar.activation(
+                    out=hid_rows[:, 2 * c + e, :],
+                    in_=hid_acc[:, e, :],
+                    func=ACT.Relu,
+                    bias=b1_cols[:, c // 2, c % 2 * 2 + e : c % 2 * 2 + e + 1],
+                )
+
+        def quantise_hid(g):
+            hid_grouped = stage.tile([P, B_TILES, P, 4], BF16, align_bytes=64, tag="grouped")
+            for bt in range(B_TILES):
+                nc.vector.tensor_copy(
+                    out=hid_grouped[:, bt, :, :],
+                    in_=hid_rows[:, 4 * g : 4 * g + 4, bt * P : (bt + 1) * P].rearrange("p t b -> p b t"),
+                )
+            for bt in range(B_TILES):
+                nc.vector.quantize_mx(
+                    out=hid_codes[:, g, bt * P : (bt + 1) * P].bitcast(FP8X4),
+                    scales=hid_scales[:, g, bt * P : (bt + 1) * P],
+                    in_=hid_grouped[:, bt, :, :].rearrange("p b t -> p (b t)"),
+                )
+
+        for g in range(PASSES2):
+            prepare_w1(2 * g)
+            prepare_w1(2 * g + 1)
+            if g > 0:
+                layer1(2 * g - 1)
+                quantise_hid(g - 1)
+            layer1(2 * g)
+
+        inv_std_p = keep.tile([P, B_TILES, Z], F32)
+
+        mu_q = keep.tile([P, B_TILES, Z], F32)
+        lv_q = keep.tile([P, B_TILES, Z], F32)
+        std_q = keep.tile([P, B_TILES, Z], F32)
+        z_sb = keep.tile([P, B_TILES, Z], F32)
+        dev = keep.tile([P, B_TILES, Z], F32)
+        lv_diff = keep.tile([P, B_TILES, Z], F32)
+        dev_sq = keep.tile([P, B_TILES, Z], BF16)
+        var_ratio = keep.tile([P, B_TILES, Z], BF16)
+
+        def kl_sum(term, part, t):
+            return kl_sums[:, term * Z_PARTS + part, t : t + 1]
+
+        def group_w2(q):
+            banks = [transpose_pass(w2_words[q], g) for g in range(PASSES2)]
+            return [group_rows_in_order(nc.scalar.copy, banks[g]) for g in range(PASSES2)]
+
+        def quantise_w2(q, g, grouped):
+            quantise(grouped[g], w2_codes[:, q, g, :], w2_scales[:, q, g, :])
+
+        def prepare_w2(q):
+            grouped = group_w2(q)
+            for g in range(PASSES2):
+                quantise_w2(q, g, grouped)
+
+        def layer2(q):
+            stats_acc = psum_acc.tile([P, B_TILES, PAIR], F32, tag="acc")
+            for t in range(B_TILES):
+                for g in range(PASSES2):
+                    nc.tensor.matmul_mx(
+                        out=stats_acc[:, t, :],
+                        lhsT=hid_codes[:, g, t * P : (t + 1) * P].bitcast(FP8X4),
+                        lhsT_scale=hid_scales[:, g, t * P : (t + 1) * P],
+                        rhs=w2_codes[:, q, g, :].bitcast(FP8X4),
+                        rhs_scale=w2_scales[:, q, g, :],
+                        start=(g == 0),
+                        stop=(g == PASSES2 - 1),
+                    )
+            return stats_acc
+
+        def bias2(q):
+            return b2_all[:, q * PAIR : (q + 1) * PAIR].unsqueeze(1).to_broadcast([P, B_TILES, PAIR])
+
+        def store(out, tile, cols):
+            nc.sync.dma_start(out=out.rearrange("(t p) z -> p t z", p=P)[:, :, cols], in_=tile[:, :, cols])
+
+        def sum_dev_squares(part):
+            cols = slice(part * PAIR, (part + 1) * PAIR)
+            for t in range(B_TILES):
+                nc.scalar.activation(
+                    out=dev_sq[:, t, cols],
+                    in_=dev[:, t, cols],
+                    func=ACT.Square,
+                    accum_out=kl_sum(DEV_SQ, part, t),
+                )
+
+        def finish_mu(part):
+            cols = slice(part * PAIR, (part + 1) * PAIR)
+            q_ahead = part + PREPARE_AHEAD
+            grouped = group_w2(q_ahead)
+            if part == 0:
+                nc.scalar.activation(out=inv_std_p[:], in_=lvp_sb[:], func=ACT.Exp, scale=-0.5)
+            stats_acc = layer2(part)
+            if part > 0:
+                sum_dev_squares(part - 1)
+            quantise_w2(q_ahead, 0, grouped)
+            nc.vector.tensor_tensor(out=mu_q[:, :, cols], in0=stats_acc[:], in1=bias2(part), op=ALU.add)
+            store(out_1, mu_q, cols)
+            quantise_w2(q_ahead, 1, grouped)
+            nc.vector.tensor_tensor(out=dev[:, :, cols], in0=mu_q[:, :, cols], in1=mup_sb[:, :, cols], op=ALU.subtract)
+            quantise_w2(q_ahead, 2, grouped)
+            nc.vector.tensor_tensor(out=dev[:, :, cols], in0=dev[:, :, cols], in1=inv_std_p[:, :, cols], op=ALU.mult)
+
+        def finish_logvar_and_sample():
+            parts = range(Z_PARTS)
+            col_ranges = [slice(part * PAIR, (part + 1) * PAIR) for part in parts]
+            stats_accs = [layer2(Z_PARTS + part) for part in parts]
+            sum_dev_squares(Z_PARTS - 1)
+            for part in parts:
+                nc.vector.tensor_tensor(
+                    out=lv_q[:, :, col_ranges[part]], in0=stats_accs[part][:], in1=bias2(Z_PARTS + part), op=ALU.add
+                )
+            for cols in col_ranges:
+                nc.vector.tensor_scalar(
+                    out=lv_q[:, :, cols], in0=lv_q[:, :, cols], scalar1=CLAMP, scalar2=-CLAMP, op0=ALU.min, op1=ALU.max
+                )
+                store(out_2, lv_q, cols)
+                nc.scalar.activation(out=std_q[:, :, cols], in_=lv_q[:, :, cols], func=ACT.Exp, scale=0.5)
+            for part in parts:
+                for t in range(B_TILES):
+                    nc.vector.scalar_tensor_tensor(
+                        out=lv_diff[:, t, col_ranges[part]],
+                        in0=lv_q[:, t, col_ranges[part]],
+                        scalar=-1.0,
+                        in1=lvp_sb[:, t, col_ranges[part]],
+                        op0=ALU.mult,
+                        op1=ALU.add,
+                        accum_out=kl_sum(LV_DIFF, part, t),
+                    )
+            for part in parts:
+                for t in range(B_TILES):
+                    nc.scalar.activation(
+                        out=var_ratio[:, t, col_ranges[part]],
+                        in_=lv_diff[:, t, col_ranges[part]],
+                        func=ACT.Exp,
+                        scale=-1.0,
+                        accum_out=kl_sum(VAR_RATIO, part, t),
+                    )
+            for cols in col_ranges:
+                nc.vector.tensor_tensor(out=z_sb[:, :, cols], in0=std_q[:, :, cols], in1=eps_sb[:, :, cols], op=ALU.mult)
+            for cols in col_ranges:
+                nc.vector.tensor_tensor(out=z_sb[:, :, cols], in0=z_sb[:, :, cols], in1=mu_q[:, :, cols], op=ALU.add)
+                store(out_0, z_sb, cols)
+
+        assert PREPARE_AHEAD == Z_PARTS
+        prepare_w2(0)
+        layer1(W1_PAIRS - 1)
+        quantise_hid(PASSES2 - 1)
+        prepare_w2(1)
+        for part in range(Z_PARTS):
+            finish_mu(part)
+        finish_logvar_and_sample()
+
+        kl_bank = psum_t.tile([P, 4 * P], F32, tag="bank")
+        for j in range(KL_TERMS * Z_PARTS):
+            nc.tensor.matmul(
+                out=kl_bank[:, 0:P],
+                lhsT=kl_sums[:, j, :],
+                rhs=ident[:],
+                start=(j == 0),
+                stop=(j == KL_TERMS * Z_PARTS - 1),
+            )
+        kl_rows = keep.tile([P, P], F32)
+        nc.scalar.activation(out=kl_rows[:], in_=kl_bank[:, 0:P], func=ACT.Copy, scale=0.5, bias=-0.5 * Z)
+        nc.sync.dma_start(out=out_3.rearrange("(t p) -> t p", p=P), in_=kl_rows[0:B_TILES, :])

@@ -24,12 +24,13 @@ W2_PAIRS = 2 * Z // PAIR
 B_TILES = B // P
 Z_PARTS = Z // PAIR
 CLAMP = 10.0
-PREPARE_AHEAD = 2
 KL_TERMS = 3
 DEV_SQ, LV_DIFF, VAR_RATIO = 0, 1, 2
 
 FLOPS = 2 * B * K1 * H + 2 * B * H * 2 * Z
 
+W1_COPY = "SVSS"
+W2_ORDER = (2, 3, 0, 1)
 
 def tile_vrnncell_pa_kernel(
     tc, x_t, h_prev, eps, enc_w1, enc_b1, enc_w2, enc_b2, mu_p, logvar_p, out_0, out_1, out_2, out_3
@@ -38,9 +39,18 @@ def tile_vrnncell_pa_kernel(
     with ExitStack() as ctx:
         keep = ctx.enter_context(tc.tile_pool(name="keep", bufs=1))
         stage = ctx.enter_context(tc.tile_pool(name="stage", bufs=6))
+        permuted = ctx.enter_context(tc.tile_pool(name="permuted", bufs=3))
         psum_t = ctx.enter_context(tc.psum_pool(name="psum_t", bufs=6))
         psum_acc = ctx.enter_context(tc.psum_pool(name="psum_acc", bufs=2))
         ctx.enter_context(tc.manual_schedule())
+
+        b1_cols = keep.tile([P, PASSES2, 4], BF16)
+        nc.scalar.dma_start(out=b1_cols[:], in_=enc_b1.rearrange("(g p t) -> p g t", p=P, t=4))
+        b2_row = keep.tile([P, 2 * Z], BF16)
+        nc.vector.memset(b2_row[:].bitcast(U32), 0)
+        warm = keep.tile([P, 1], F32)
+        nc.vector.memset(warm[:], 0.0)
+        nc.scalar.activation(out=warm[:], in_=warm[:], func=ACT.Exp)
 
         def load_rows(rows, width, name):
             raw = keep.tile([P, 2 * width], BF16, name=name)
@@ -56,6 +66,7 @@ def tile_vrnncell_pa_kernel(
 
         x_words = load_pair(x_t, O, "x_raw")
         h_words = load_pair(h_prev, H, "h_raw")
+        nc.sync.dma_start(out=b2_row[0:1, :], in_=enc_b2.rearrange("(o n) -> o n", o=1))
         w1_words = [load_w1_pair(c) for c in range(W1_PAIRS)]
 
         def load_prior(src, name):
@@ -66,28 +77,14 @@ def tile_vrnncell_pa_kernel(
         lvp_sb = load_prior(logvar_p, "lvp_sb")
         mup_sb = load_prior(mu_p, "mup_sb")
         eps_sb = load_prior(eps, "eps_sb")
-        w2_words = [
-            load_pair(enc_w2[q * PAIR : (q + 1) * PAIR, :], H, "w2_raw%d" % q) for q in range(W2_PAIRS)
-        ]
+        w2_words = {q: load_pair(enc_w2[q * PAIR : (q + 1) * PAIR, :], H, "w2_raw%d" % q) for q in W2_ORDER}
 
         ident = keep.tile([P, P], F32)
         make_identity(nc, ident[:])
         ones = keep.tile([P, P], BF16)
         nc.gpsimd.memset(ones[:], 1.0)
-        b1_rows = keep.tile([P, PAIR], F32)
-        nc.gpsimd.memset(b1_rows[:], 0.0)
-        nc.scalar.dma_start(
-            out=b1_rows[:].bitcast(BF16)[0:PASSES2, :], in_=enc_b1.rearrange("(g w) -> g w", g=PASSES2)
-        )
-        b2_row = keep.tile([P, 2 * Z], BF16)
-        nc.gpsimd.memset(b2_row[:], 0.0)
-        nc.scalar.dma_start(out=b2_row[0:1, :], in_=enc_b2.rearrange("(o n) -> o n", o=1))
         kl_sums = keep.tile([P, KL_TERMS * Z_PARTS, P], F32)
         nc.gpsimd.memset(kl_sums[:], 0.0)
-
-        warm = keep.tile([P, 1], F32)
-        nc.vector.memset(warm[:], 0.0)
-        nc.scalar.activation(out=warm[:], in_=warm[:], func=ACT.Exp)
 
         x_codes = keep.tile([P, PASSES1, B], U32, align_bytes=64)
         x_scales = keep.tile([P, PASSES1, B], U8, align_bytes=64)
@@ -98,28 +95,37 @@ def tile_vrnncell_pa_kernel(
         w2_codes = keep.tile([P, W2_PAIRS, PASSES2, PAIR], U32, align_bytes=64)
         w2_scales = keep.tile([P, W2_PAIRS, PASSES2, PAIR], U8, align_bytes=64)
 
-        def transpose_pass(words, g):
+        copies = {"V": nc.vector.tensor_copy, "S": nc.scalar.copy}
+
+        def permute_row(engine, words, a, passes):
+            row = permuted.tile([P, passes, 2, P], F32, tag="row%d" % passes)
+            copies[engine](out=row[:], in_=words[:, a, :].rearrange("p (g w u) -> p g u w", g=passes, u=2))
+            return row
+
+        def transpose_pass(words, g, rows_permuted=None):
             bank = psum_t.tile([P, 4 * P], F32)
-            for a in range(2):
+            for a in (1, 0):
                 for u in range(2):
+                    if a == 0 and rows_permuted is not None:
+                        in_ap = rows_permuted[:, g, u, :]
+                    else:
+                        in_ap = words[:, a, 2 * g * P + u : 2 * (g + 1) * P : 2]
                     nc.tensor.transpose(
-                        out=bank[:, (2 * a + u) * P : (2 * a + u + 1) * P],
-                        in_=words[:, a, 2 * g * P + u : 2 * (g + 1) * P : 2],
-                        identity=ident[:],
+                        out=bank[:, (2 * a + u) * P : (2 * a + u + 1) * P], in_=in_ap, identity=ident[:]
                     )
             return bank
 
-        def group_rows_in_order(copy, bank):
+        def group_rows_in_order(engine, bank):
             grouped = stage.tile([P, 4 * PAIR], BF16, align_bytes=64)
-            copy(
+            copies[engine](
                 out=grouped[:].bitcast(F32).rearrange("p (r a u) -> p r a u", a=2, u=2),
                 in_=bank[:].rearrange("p (a u r) -> p r a u", a=2, u=2),
             )
             return grouped
 
-        def group_rows_even_odd(copy, bank):
+        def group_rows_even_odd(engine, bank):
             grouped = stage.tile([P, 4 * PAIR], BF16, align_bytes=64)
-            copy(
+            copies[engine](
                 out=grouped[:].bitcast(F32).rearrange("p (a r u) -> p a r u", a=2, u=2),
                 in_=bank[:].rearrange("p (a u r) -> p a r u", a=2, u=2),
             )
@@ -129,41 +135,22 @@ def tile_vrnncell_pa_kernel(
             nc.vector.quantize_mx(out=codes.bitcast(FP8X4), scales=scales, in_=grouped[:])
 
         x_banks = [transpose_pass(x_words, 0)] + [transpose_pass(h_words, g) for g in range(PASSES1 - 1)]
-        x_grouped = [
-            group_rows_in_order(nc.vector.tensor_copy if g % 2 == 0 else nc.scalar.copy, x_banks[g])
-            for g in range(PASSES1)
-        ]
+        x_grouped = [group_rows_in_order("VS"[g % 2], x_banks[g]) for g in range(PASSES1)]
         for g in range(PASSES1):
             quantise(x_grouped[g], x_codes[:, g, :], x_scales[:, g, :])
 
-        b1_bank = psum_t.tile([P, 4 * P], F32, tag="bank")
-        for h in range(2):
-            nc.tensor.transpose(out=b1_bank[:, h * P : (h + 1) * P], in_=b1_rows[:, h::2], identity=ident[:])
-        b1_cols = keep.tile([P, PASSES2, 4], F32)
-        for h in range(2):
-            nc.vector.tensor_copy(
-                out=b1_cols[:, :, 2 * h : 2 * h + 2],
-                in_=b1_bank[:].bitcast(BF16)[:, h * PAIR : h * PAIR + 2 * PASSES2].rearrange("p (g e) -> p g e", e=2),
-            )
-
         b2_all = keep.tile([P, 2 * Z], F32)
-        for half in range(2):
-            b2_bank = psum_acc.tile([P, Z], F32, tag="acc")
-            nc.tensor.matmul(
-                out=b2_bank[:], lhsT=ones[:], rhs=b2_row[:, half * Z : (half + 1) * Z], start=True, stop=True
-            )
-            nc.vector.tensor_copy(out=b2_all[:, half * Z : (half + 1) * Z], in_=b2_bank[:])
+
+        def spread_b2():
+            for half in range(2):
+                b2_bank = psum_acc.tile([P, Z], F32, tag="acc")
+                nc.tensor.matmul(
+                    out=b2_bank[:], lhsT=ones[:], rhs=b2_row[:, half * Z : (half + 1) * Z], start=True, stop=True
+                )
+                nc.scalar.copy(out=b2_all[:, half * Z : (half + 1) * Z], in_=b2_bank[:])
 
         hid_rows = keep.tile([P, 2 * W1_PAIRS, B], BF16)
-
-        def prepare_w1(c):
-            banks = [transpose_pass(w1_words[c], g) for g in range(PASSES1)]
-            grouped = [
-                group_rows_even_odd(nc.vector.tensor_copy if g == PASSES1 - 1 else nc.scalar.copy, banks[g])
-                for g in range(PASSES1)
-            ]
-            for g in range(PASSES1):
-                quantise(grouped[g], w1_codes[:, c, g, :], w1_scales[:, c, g, :])
+        inv_std_p = keep.tile([P, B_TILES, Z], F32)
 
         def layer1(c):
             hid_acc = psum_acc.tile([P, 2, B], F32, tag="acc")
@@ -179,12 +166,18 @@ def tile_vrnncell_pa_kernel(
                         stop=(g == PASSES1 - 1),
                     )
             for e in range(2):
-                nc.scalar.activation(
-                    out=hid_rows[:, 2 * c + e, :],
-                    in_=hid_acc[:, e, :],
-                    func=ACT.Relu,
-                    bias=b1_cols[:, c // 2, c % 2 * 2 + e : c % 2 * 2 + e + 1],
-                )
+                bias = b1_cols[:, c // 2, c % 2 * 2 + e : c % 2 * 2 + e + 1]
+                if c == W1_PAIRS - 1 and e == 1:
+                    nc.vector.tensor_scalar(
+                        out=hid_rows[:, 2 * c + e, :],
+                        in0=hid_acc[:, e, :],
+                        scalar1=bias,
+                        scalar2=0.0,
+                        op0=ALU.add,
+                        op1=ALU.max,
+                    )
+                else:
+                    nc.scalar.activation(out=hid_rows[:, 2 * c + e, :], in_=hid_acc[:, e, :], func=ACT.Relu, bias=bias)
 
         def quantise_hid(g):
             hid_grouped = stage.tile([P, B_TILES, P, 4], BF16, align_bytes=64, tag="grouped")
@@ -200,15 +193,22 @@ def tile_vrnncell_pa_kernel(
                     in_=hid_grouped[:, bt, :, :].rearrange("p b t -> p (b t)"),
                 )
 
-        for g in range(PASSES2):
-            prepare_w1(2 * g)
-            prepare_w1(2 * g + 1)
-            if g > 0:
-                layer1(2 * g - 1)
-                quantise_hid(g - 1)
-            layer1(2 * g)
-
-        inv_std_p = keep.tile([P, B_TILES, Z], F32)
+        row0 = {0: None}
+        for c in range(W1_PAIRS):
+            banks = [transpose_pass(w1_words[c], g, row0[c]) for g in range(PASSES1)]
+            grouped = [group_rows_even_odd(W1_COPY[g], banks[g]) for g in range(PASSES1)]
+            if c == 0:
+                spread_b2()
+            if c % 2 == 1 and c > 1:
+                quantise_hid(c // 2 - 1)
+            for g in range(PASSES1):
+                quantise(grouped[g], w1_codes[:, c, g, :], w1_scales[:, c, g, :])
+                if g == 1 and c + 1 < W1_PAIRS:
+                    row0[c + 1] = permute_row("V", w1_words[c + 1], 0, PASSES1)
+            if c > 0:
+                layer1(c - 1)
+            if c == 4:
+                nc.scalar.activation(out=inv_std_p[:], in_=lvp_sb[:], func=ACT.Exp, scale=-0.5)
 
         mu_q = keep.tile([P, B_TILES, Z], F32)
         lv_q = keep.tile([P, B_TILES, Z], F32)
@@ -222,17 +222,15 @@ def tile_vrnncell_pa_kernel(
         def kl_sum(term, part, t):
             return kl_sums[:, term * Z_PARTS + part, t : t + 1]
 
+        def cols_of(part):
+            return slice(part * PAIR, (part + 1) * PAIR)
+
         def group_w2(q):
             banks = [transpose_pass(w2_words[q], g) for g in range(PASSES2)]
-            return [group_rows_in_order(nc.scalar.copy, banks[g]) for g in range(PASSES2)]
+            return [group_rows_in_order("S", banks[g]) for g in range(PASSES2)]
 
         def quantise_w2(q, g, grouped):
             quantise(grouped[g], w2_codes[:, q, g, :], w2_scales[:, q, g, :])
-
-        def prepare_w2(q):
-            grouped = group_w2(q)
-            for g in range(PASSES2):
-                quantise_w2(q, g, grouped)
 
         def layer2(q):
             stats_acc = psum_acc.tile([P, B_TILES, PAIR], F32, tag="acc")
@@ -249,98 +247,110 @@ def tile_vrnncell_pa_kernel(
                     )
             return stats_acc
 
-        def bias2(q):
-            return b2_all[:, q * PAIR : (q + 1) * PAIR].unsqueeze(1).to_broadcast([P, B_TILES, PAIR])
+        def add_bias(out, stats_acc, q, part):
+            bias = b2_all[:, q * PAIR : (q + 1) * PAIR].unsqueeze(1).to_broadcast([P, B_TILES, PAIR])
+            nc.vector.tensor_tensor(out=out[:, :, cols_of(part)], in0=stats_acc[:], in1=bias, op=ALU.add)
 
-        def store(out, tile, cols):
+        def store(out, tile, part):
+            cols = cols_of(part)
             nc.sync.dma_start(out=out.rearrange("(t p) z -> p t z", p=P)[:, :, cols], in_=tile[:, :, cols])
 
-        def sum_dev_squares(part):
-            cols = slice(part * PAIR, (part + 1) * PAIR)
+        def combine(out, in0, in1, op, part):
+            cols = cols_of(part)
+            nc.vector.tensor_tensor(out=out[:, :, cols], in0=in0[:, :, cols], in1=in1[:, :, cols], op=op)
+
+        def clip_and_std(part):
+            cols = cols_of(part)
+            nc.vector.tensor_scalar(
+                out=lv_q[:, :, cols], in0=lv_q[:, :, cols], scalar1=CLAMP, scalar2=-CLAMP, op0=ALU.min, op1=ALU.max
+            )
+            store(out_2, lv_q, part)
+            nc.scalar.activation(out=std_q[:, :, cols], in_=lv_q[:, :, cols], func=ACT.Exp, scale=0.5)
+
+        def sum_lv_diff(part):
+            for t in range(B_TILES):
+                nc.vector.scalar_tensor_tensor(
+                    out=lv_diff[:, t, cols_of(part)],
+                    in0=lv_q[:, t, cols_of(part)],
+                    scalar=-1.0,
+                    in1=lvp_sb[:, t, cols_of(part)],
+                    op0=ALU.mult,
+                    op1=ALU.add,
+                    accum_out=kl_sum(LV_DIFF, part, t),
+                )
+
+        def sum_var_ratio(part):
             for t in range(B_TILES):
                 nc.scalar.activation(
-                    out=dev_sq[:, t, cols],
-                    in_=dev[:, t, cols],
+                    out=var_ratio[:, t, cols_of(part)],
+                    in_=lv_diff[:, t, cols_of(part)],
+                    func=ACT.Exp,
+                    scale=-1.0,
+                    accum_out=kl_sum(VAR_RATIO, part, t),
+                )
+
+        def sum_dev_squares(part):
+            for t in range(B_TILES):
+                nc.scalar.activation(
+                    out=dev_sq[:, t, cols_of(part)],
+                    in_=dev[:, t, cols_of(part)],
                     func=ACT.Square,
                     accum_out=kl_sum(DEV_SQ, part, t),
                 )
 
-        def finish_mu(part):
-            cols = slice(part * PAIR, (part + 1) * PAIR)
-            q_ahead = part + PREPARE_AHEAD
-            grouped = group_w2(q_ahead)
-            if part == 0:
-                nc.scalar.activation(out=inv_std_p[:], in_=lvp_sb[:], func=ACT.Exp, scale=-0.5)
-            stats_acc = layer2(part)
-            if part > 0:
-                sum_dev_squares(part - 1)
-            quantise_w2(q_ahead, 0, grouped)
-            nc.vector.tensor_tensor(out=mu_q[:, :, cols], in0=stats_acc[:], in1=bias2(part), op=ALU.add)
-            store(out_1, mu_q, cols)
-            quantise_w2(q_ahead, 1, grouped)
-            nc.vector.tensor_tensor(out=dev[:, :, cols], in0=mu_q[:, :, cols], in1=mup_sb[:, :, cols], op=ALU.subtract)
-            quantise_w2(q_ahead, 2, grouped)
-            nc.vector.tensor_tensor(out=dev[:, :, cols], in0=dev[:, :, cols], in1=inv_std_p[:, :, cols], op=ALU.mult)
+        lv_pairs = W2_ORDER[:Z_PARTS]
+        mu_pairs = W2_ORDER[Z_PARTS:]
 
-        def finish_logvar_and_sample():
-            parts = range(Z_PARTS)
-            col_ranges = [slice(part * PAIR, (part + 1) * PAIR) for part in parts]
-            stats_accs = [layer2(Z_PARTS + part) for part in parts]
-            sum_dev_squares(Z_PARTS - 1)
-            for part in parts:
-                nc.vector.tensor_tensor(
-                    out=lv_q[:, :, col_ranges[part]], in0=stats_accs[part][:], in1=bias2(Z_PARTS + part), op=ALU.add
-                )
-            for cols in col_ranges:
-                nc.vector.tensor_scalar(
-                    out=lv_q[:, :, cols], in0=lv_q[:, :, cols], scalar1=CLAMP, scalar2=-CLAMP, op0=ALU.min, op1=ALU.max
-                )
-                store(out_2, lv_q, cols)
-                nc.scalar.activation(out=std_q[:, :, cols], in_=lv_q[:, :, cols], func=ACT.Exp, scale=0.5)
-            for part in parts:
-                for t in range(B_TILES):
-                    nc.vector.scalar_tensor_tensor(
-                        out=lv_diff[:, t, col_ranges[part]],
-                        in0=lv_q[:, t, col_ranges[part]],
-                        scalar=-1.0,
-                        in1=lvp_sb[:, t, col_ranges[part]],
-                        op0=ALU.mult,
-                        op1=ALU.add,
-                        accum_out=kl_sum(LV_DIFF, part, t),
-                    )
-            for part in parts:
-                for t in range(B_TILES):
-                    nc.scalar.activation(
-                        out=var_ratio[:, t, col_ranges[part]],
-                        in_=lv_diff[:, t, col_ranges[part]],
-                        func=ACT.Exp,
-                        scale=-1.0,
-                        accum_out=kl_sum(VAR_RATIO, part, t),
-                    )
-            for cols in col_ranges:
-                nc.vector.tensor_tensor(out=z_sb[:, :, cols], in0=std_q[:, :, cols], in1=eps_sb[:, :, cols], op=ALU.mult)
-            for cols in col_ranges:
-                nc.vector.tensor_tensor(out=z_sb[:, :, cols], in0=z_sb[:, :, cols], in1=mu_q[:, :, cols], op=ALU.add)
-                store(out_0, z_sb, cols)
-
-        assert PREPARE_AHEAD == Z_PARTS
-        prepare_w2(0)
+        grouped = group_w2(lv_pairs[0])
+        for g in range(PASSES2):
+            quantise_w2(lv_pairs[0], g, grouped)
         layer1(W1_PAIRS - 1)
         quantise_hid(PASSES2 - 1)
-        prepare_w2(1)
+        for q in (lv_pairs[1], mu_pairs[0]):
+            grouped = group_w2(q)
+            for g in range(PASSES2):
+                quantise_w2(q, g, grouped)
+        lv_accs = [layer2(q) for q in lv_pairs]
         for part in range(Z_PARTS):
-            finish_mu(part)
-        finish_logvar_and_sample()
+            add_bias(lv_q, lv_accs[part], lv_pairs[part], part)
+        for part in range(Z_PARTS):
+            clip_and_std(part)
+        grouped = group_w2(mu_pairs[1])
+        quantise_w2(mu_pairs[1], 0, grouped)
+        sum_lv_diff(0)
+        quantise_w2(mu_pairs[1], 1, grouped)
+        sum_lv_diff(1)
+        quantise_w2(mu_pairs[1], 2, grouped)
+        for part in range(Z_PARTS):
+            sum_var_ratio(part)
+            combine(z_sb, std_q, eps_sb, ALU.mult, part)
+
+        stats_accs = [layer2(q) for q in mu_pairs]
+        add_bias(mu_q, stats_accs[0], mu_pairs[0], 0)
+        store(out_1, mu_q, 0)
+        combine(dev, mu_q, mup_sb, ALU.subtract, 0)
+        add_bias(mu_q, stats_accs[1], mu_pairs[1], 1)
+        store(out_1, mu_q, 1)
+        combine(dev, dev, inv_std_p, ALU.mult, 0)
+        sum_dev_squares(0)
+        combine(dev, mu_q, mup_sb, ALU.subtract, 1)
+        combine(z_sb, z_sb, mu_q, ALU.add, 0)
+        store(out_0, z_sb, 0)
+        combine(dev, dev, inv_std_p, ALU.mult, 1)
+        sum_dev_squares(1)
+        combine(z_sb, z_sb, mu_q, ALU.add, 1)
+        store(out_0, z_sb, 1)
 
         kl_bank = psum_t.tile([P, 4 * P], F32, tag="bank")
-        for j in range(KL_TERMS * Z_PARTS):
+        kl_order = [term * Z_PARTS + part for term in (LV_DIFF, VAR_RATIO, DEV_SQ) for part in range(Z_PARTS)]
+        for j in kl_order:
             nc.tensor.matmul(
                 out=kl_bank[:, 0:P],
                 lhsT=kl_sums[:, j, :],
                 rhs=ident[:],
-                start=(j == 0),
-                stop=(j == KL_TERMS * Z_PARTS - 1),
+                start=(j == kl_order[0]),
+                stop=(j == kl_order[-1]),
             )
         kl_rows = keep.tile([P, P], F32)
         nc.scalar.activation(out=kl_rows[:], in_=kl_bank[:, 0:P], func=ACT.Copy, scale=0.5, bias=-0.5 * Z)
-        nc.sync.dma_start(out=out_3.rearrange("(t p) -> t p", p=P), in_=kl_rows[0:B_TILES, :])
+        nc.scalar.dma_start(out=out_3.rearrange("(t p) -> t p", p=P), in_=kl_rows[0:B_TILES, :])

@@ -44,8 +44,8 @@ def tile_vrnncell_pa_kernel(
         psum_acc = ctx.enter_context(tc.psum_pool(name="psum_acc", bufs=2))
         ctx.enter_context(tc.manual_schedule())
 
-        b1_cols = keep.tile([P, PASSES2, 4], BF16)
-        nc.scalar.dma_start(out=b1_cols[:], in_=enc_b1.rearrange("(g p t) -> p g t", p=P, t=4))
+        ones = keep.tile([P, Z], BF16)
+        nc.vector.memset(ones[:], 1.0)
         b2_row = keep.tile([P, 2 * Z], BF16)
         nc.vector.memset(b2_row[:].bitcast(U32), 0)
         warm = keep.tile([P, 1], F32)
@@ -66,6 +66,8 @@ def tile_vrnncell_pa_kernel(
 
         x_words = load_pair(x_t, O, "x_raw")
         h_words = load_pair(h_prev, H, "h_raw")
+        b1_cols = keep.tile([P, PASSES2, 4], BF16)
+        nc.sync.dma_start(out=b1_cols[:], in_=enc_b1.rearrange("(g p t) -> p g t", p=P, t=4))
         nc.sync.dma_start(out=b2_row[0:1, :], in_=enc_b2.rearrange("(o n) -> o n", o=1))
         w1_words = [load_w1_pair(c) for c in range(W1_PAIRS)]
 
@@ -81,8 +83,6 @@ def tile_vrnncell_pa_kernel(
 
         ident = keep.tile([P, P], F32)
         make_identity(nc, ident[:])
-        ones = keep.tile([P, P], BF16)
-        nc.gpsimd.memset(ones[:], 1.0)
         kl_sums = keep.tile([P, KL_TERMS * Z_PARTS, P], F32)
         nc.gpsimd.memset(kl_sums[:], 0.0)
 
@@ -134,6 +134,12 @@ def tile_vrnncell_pa_kernel(
         def quantise(grouped, codes, scales):
             nc.vector.quantize_mx(out=codes.bitcast(FP8X4), scales=scales, in_=grouped[:])
 
+        def keep_clock_up(count):
+            for n in range(count):
+                unread = psum_acc.tile([P, Z], F32, tag="acc")
+                nc.tensor.matmul(out=unread[:], lhsT=ones[:, 0:P], rhs=ones[:], start=True, stop=True)
+
+        keep_clock_up(4)
         x_banks = [transpose_pass(x_words, 0)] + [transpose_pass(h_words, g) for g in range(PASSES1 - 1)]
         x_grouped = [group_rows_in_order("VS"[g % 2], x_banks[g]) for g in range(PASSES1)]
         for g in range(PASSES1):
@@ -145,39 +151,29 @@ def tile_vrnncell_pa_kernel(
             for half in range(2):
                 b2_bank = psum_acc.tile([P, Z], F32, tag="acc")
                 nc.tensor.matmul(
-                    out=b2_bank[:], lhsT=ones[:], rhs=b2_row[:, half * Z : (half + 1) * Z], start=True, stop=True
+                    out=b2_bank[:], lhsT=ones[:, 0:P], rhs=b2_row[:, half * Z : (half + 1) * Z], start=True, stop=True
                 )
                 nc.scalar.copy(out=b2_all[:, half * Z : (half + 1) * Z], in_=b2_bank[:])
 
         hid_rows = keep.tile([P, 2 * W1_PAIRS, B], BF16)
         inv_std_p = keep.tile([P, B_TILES, Z], F32)
 
-        def layer1(c):
-            hid_acc = psum_acc.tile([P, 2, B], F32, tag="acc")
-            for e in range(2):
-                for g in range(PASSES1):
-                    nc.tensor.matmul_mx(
-                        out=hid_acc[:, e, :],
-                        lhsT=w1_codes[:, c, g, e * P : (e + 1) * P].bitcast(FP8X4),
-                        lhsT_scale=w1_scales[:, c, g, e * P : (e + 1) * P],
-                        rhs=x_codes[:, g, :].bitcast(FP8X4),
-                        rhs_scale=x_scales[:, g, :],
-                        start=(g == 0),
-                        stop=(g == PASSES1 - 1),
-                    )
-            for e in range(2):
-                bias = b1_cols[:, c // 2, c % 2 * 2 + e : c % 2 * 2 + e + 1]
-                if c == W1_PAIRS - 1 and e == 1:
-                    nc.vector.tensor_scalar(
-                        out=hid_rows[:, 2 * c + e, :],
-                        in0=hid_acc[:, e, :],
-                        scalar1=bias,
-                        scalar2=0.0,
-                        op0=ALU.add,
-                        op1=ALU.max,
-                    )
-                else:
-                    nc.scalar.activation(out=hid_rows[:, 2 * c + e, :], in_=hid_acc[:, e, :], func=ACT.Relu, bias=bias)
+        def layer1(m):
+            c, e = m // 2, m % 2
+            hid_acc = psum_acc.tile([P, B], F32, tag="acc")
+            for g in range(PASSES1):
+                nc.tensor.matmul_mx(
+                    out=hid_acc[:],
+                    lhsT=w1_codes[:, c, g, e * P : (e + 1) * P].bitcast(FP8X4),
+                    lhsT_scale=w1_scales[:, c, g, e * P : (e + 1) * P],
+                    rhs=x_codes[:, g, :].bitcast(FP8X4),
+                    rhs_scale=x_scales[:, g, :],
+                    start=(g == 0),
+                    stop=(g == PASSES1 - 1),
+                )
+            nc.scalar.activation(
+                out=hid_rows[:, m, :], in_=hid_acc[:], func=ACT.Relu, bias=b1_cols[:, m // 4, m % 4 : m % 4 + 1]
+            )
 
         def quantise_hid(g):
             hid_grouped = stage.tile([P, B_TILES, P, 4], BF16, align_bytes=64, tag="grouped")
@@ -194,20 +190,32 @@ def tile_vrnncell_pa_kernel(
                 )
 
         row0 = {0: None}
-        for c in range(W1_PAIRS):
-            banks = [transpose_pass(w1_words[c], g, row0[c]) for g in range(PASSES1)]
-            grouped = [group_rows_even_odd(W1_COPY[g], banks[g]) for g in range(PASSES1)]
-            if c == 0:
+        waiting = []
+
+        def quantise_waiting():
+            for args in waiting:
+                quantise(*args)
+            waiting.clear()
+
+        for i in range(2 * W1_PAIRS):
+            c, half = i // 2, i % 2
+            passes = (2 * half, 2 * half + 1)
+            banks = [transpose_pass(w1_words[c], g, row0[c]) for g in passes]
+            grouped = [group_rows_even_odd(W1_COPY[g], bank) for g, bank in zip(passes, banks)]
+            if half == 1 and c + 1 < W1_PAIRS:
+                row0[c + 1] = permute_row("V", w1_words[c + 1], 0, PASSES1)
+            quantise_waiting()
+            for g, group in zip(passes, grouped):
+                waiting.append((group, w1_codes[:, c, g, :], w1_scales[:, c, g, :]))
+            if i == 0:
                 spread_b2()
-            if c % 2 == 1 and c > 1:
-                quantise_hid(c // 2 - 1)
-            for g in range(PASSES1):
-                quantise(grouped[g], w1_codes[:, c, g, :], w1_scales[:, c, g, :])
-                if g == 1 and c + 1 < W1_PAIRS:
-                    row0[c + 1] = permute_row("V", w1_words[c + 1], 0, PASSES1)
-            if c > 0:
-                layer1(c - 1)
-            if c == 4:
+            if i in (1, 2):
+                keep_clock_up(2)
+            if i in (7, 11):
+                quantise_hid(i // 4 - 1)
+            if i >= 3:
+                layer1(i - 3)
+            if i == 8:
                 nc.scalar.activation(out=inv_std_p[:], in_=lvp_sb[:], func=ACT.Exp, scale=-0.5)
 
         mu_q = keep.tile([P, B_TILES, Z], F32)
@@ -225,12 +233,12 @@ def tile_vrnncell_pa_kernel(
         def cols_of(part):
             return slice(part * PAIR, (part + 1) * PAIR)
 
-        def group_w2(q):
-            banks = [transpose_pass(w2_words[q], g) for g in range(PASSES2)]
-            return [group_rows_in_order("S", banks[g]) for g in range(PASSES2)]
-
-        def quantise_w2(q, g, grouped):
-            quantise(grouped[g], w2_codes[:, q, g, :], w2_scales[:, q, g, :])
+        def group_w2(units):
+            banks = [transpose_pass(w2_words[q], g) for q, g in units]
+            grouped = [group_rows_in_order("S", bank) for bank in banks]
+            quantise_waiting()
+            for (q, g), group in zip(units, grouped):
+                waiting.append((group, w2_codes[:, q, g, :], w2_scales[:, q, g, :]))
 
         def layer2(q):
             stats_acc = psum_acc.tile([P, B_TILES, PAIR], F32, tag="acc")
@@ -301,29 +309,34 @@ def tile_vrnncell_pa_kernel(
         lv_pairs = W2_ORDER[:Z_PARTS]
         mu_pairs = W2_ORDER[Z_PARTS:]
 
-        grouped = group_w2(lv_pairs[0])
-        for g in range(PASSES2):
-            quantise_w2(lv_pairs[0], g, grouped)
-        layer1(W1_PAIRS - 1)
+        (lv0, lv1), (mu0, mu1) = lv_pairs, mu_pairs
+        group_w2([(lv0, 0), (lv0, 1)])
+        layer1(9)
+        group_w2([(lv0, 2), (lv1, 0)])
+        layer1(10)
+        group_w2([(lv1, 1), (lv1, 2)])
+        layer1(11)
+        group_w2([(mu0, 0), (mu0, 1), (mu0, 2)])
         quantise_hid(PASSES2 - 1)
-        for q in (lv_pairs[1], mu_pairs[0]):
-            grouped = group_w2(q)
-            for g in range(PASSES2):
-                quantise_w2(q, g, grouped)
-        lv_accs = [layer2(q) for q in lv_pairs]
-        for part in range(Z_PARTS):
-            add_bias(lv_q, lv_accs[part], lv_pairs[part], part)
-        for part in range(Z_PARTS):
-            clip_and_std(part)
-        grouped = group_w2(mu_pairs[1])
-        quantise_w2(mu_pairs[1], 0, grouped)
+        quantise_waiting()
+        lv_accs = [layer2(lv0)]
+        add_bias(lv_q, lv_accs[0], lv0, 0)
+        group_w2([(mu1, 0), (mu1, 1)])
+        lv_accs.append(layer2(lv1))
+        quantise(*waiting[0])
+        clip_and_std(0)
+        quantise(*waiting[1])
+        add_bias(lv_q, lv_accs[1], lv1, 1)
+        waiting.clear()
+        group_w2([(mu1, 2)])
         sum_lv_diff(0)
-        quantise_w2(mu_pairs[1], 1, grouped)
+        quantise_waiting()
+        clip_and_std(1)
+        sum_var_ratio(0)
+        combine(z_sb, std_q, eps_sb, ALU.mult, 0)
         sum_lv_diff(1)
-        quantise_w2(mu_pairs[1], 2, grouped)
-        for part in range(Z_PARTS):
-            sum_var_ratio(part)
-            combine(z_sb, std_q, eps_sb, ALU.mult, part)
+        sum_var_ratio(1)
+        combine(z_sb, std_q, eps_sb, ALU.mult, 1)
 
         stats_accs = [layer2(q) for q in mu_pairs]
         add_bias(mu_q, stats_accs[0], mu_pairs[0], 0)

@@ -29,7 +29,7 @@ DEV_SQ, LV_DIFF, VAR_RATIO = 0, 1, 2
 
 FLOPS = 2 * B * K1 * H + 2 * B * H * 2 * Z
 
-W1_COPY = "SVSS"
+W1_COPY = "SSSS"
 W2_ORDER = (2, 3, 0, 1)
 
 def tile_vrnncell_pa_kernel(
@@ -39,7 +39,7 @@ def tile_vrnncell_pa_kernel(
     with ExitStack() as ctx:
         keep = ctx.enter_context(tc.tile_pool(name="keep", bufs=1))
         stage = ctx.enter_context(tc.tile_pool(name="stage", bufs=6))
-        permuted = ctx.enter_context(tc.tile_pool(name="permuted", bufs=3))
+        permuted = ctx.enter_context(tc.tile_pool(name="permuted", bufs=4))
         psum_t = ctx.enter_context(tc.psum_pool(name="psum_t", bufs=6))
         psum_acc = ctx.enter_context(tc.psum_pool(name="psum_acc", bufs=2))
         ctx.enter_context(tc.manual_schedule())
@@ -52,20 +52,22 @@ def tile_vrnncell_pa_kernel(
         nc.vector.memset(warm[:], 0.0)
         nc.scalar.activation(out=warm[:], in_=warm[:], func=ACT.Exp)
 
-        def load_rows(rows, width, name):
+        def load_rows(rows, width, name, cuts=()):
             raw = keep.tile([P, 2 * width], BF16, name=name)
-            nc.sync.dma_start(out=raw[:].rearrange("p (a k) -> p a k", a=2), in_=rows)
+            edges = (0,) + cuts + (width,)
+            for lo, hi in zip(edges[:-1], edges[1:]):
+                nc.sync.dma_start(out=raw[:].rearrange("p (a k) -> p a k", a=2)[:, :, lo:hi], in_=rows[:, :, lo:hi])
             return raw[:].bitcast(F32).rearrange("p (a w) -> p a w", a=2)
 
-        def load_pair(rows, width, name):
-            return load_rows(rows.rearrange("(p a) k -> p a k", a=2), width, name)
+        def load_pair(rows, width, name, cuts=()):
+            return load_rows(rows.rearrange("(p a) k -> p a k", a=2), width, name, cuts)
 
         def load_w1_pair(c):
             quad = enc_w1[c // 2 * K_PASS : (c // 2 + 1) * K_PASS, :].rearrange("(p t) k -> p t k", t=4)
-            return load_rows(quad[:, c % 2 * 2 : c % 2 * 2 + 2, :], K1, "w1_raw%d" % c)
+            return load_rows(quad[:, c % 2 * 2 : c % 2 * 2 + 2, :], K1, "w1_raw%d" % c, (K1 // 2,) if c < 2 else ())
 
         x_words = load_pair(x_t, O, "x_raw")
-        h_words = load_pair(h_prev, H, "h_raw")
+        h_words = load_pair(h_prev, H, "h_raw", (K_PASS,))
         b1_cols = keep.tile([P, PASSES2, 4], BF16)
         nc.sync.dma_start(out=b1_cols[:], in_=enc_b1.rearrange("(g p t) -> p g t", p=P, t=4))
         nc.sync.dma_start(out=b2_row[0:1, :], in_=enc_b2.rearrange("(o n) -> o n", o=1))
@@ -97,19 +99,25 @@ def tile_vrnncell_pa_kernel(
 
         copies = {"V": nc.vector.tensor_copy, "S": nc.scalar.copy}
 
-        def permute_row(engine, words, a, passes):
-            row = permuted.tile([P, passes, 2, P], F32, tag="row%d" % passes)
-            copies[engine](out=row[:], in_=words[:, a, :].rearrange("p (g w u) -> p g u w", g=passes, u=2))
-            return row
+        def permute_half(words, first, passes):
+            rows = permuted.tile([P, 2, 2, 2, P], F32, tag="rows")
+            for a in range(2):
+                nc.vector.tensor_copy(
+                    out=rows[:, a, 0:passes, :, :],
+                    in_=words[:, a, first * PAIR : (first + passes) * PAIR].rearrange(
+                        "p (g w u) -> p g u w", g=passes, u=2
+                    ),
+                )
+            return rows
 
-        def transpose_pass(words, g, rows_permuted=None):
+        def transpose_pass(words, g, rows=None):
             bank = psum_t.tile([P, 4 * P], F32)
-            for a in (1, 0):
+            for a in range(2):
                 for u in range(2):
-                    if a == 0 and rows_permuted is not None:
-                        in_ap = rows_permuted[:, g, u, :]
-                    else:
+                    if rows is None:
                         in_ap = words[:, a, 2 * g * P + u : 2 * (g + 1) * P : 2]
+                    else:
+                        in_ap = rows[:, a, g % 2, u, :]
                     nc.tensor.transpose(
                         out=bank[:, (2 * a + u) * P : (2 * a + u + 1) * P], in_=in_ap, identity=ident[:]
                     )
@@ -189,7 +197,9 @@ def tile_vrnncell_pa_kernel(
                     in_=hid_grouped[:, bt, :, :].rearrange("p b t -> p (b t)"),
                 )
 
-        row0 = {0: None}
+        lv_pairs = W2_ORDER[:Z_PARTS]
+        mu_pairs = W2_ORDER[Z_PARTS:]
+        halves = {}
         waiting = []
 
         def quantise_waiting():
@@ -197,20 +207,26 @@ def tile_vrnncell_pa_kernel(
                 quantise(*args)
             waiting.clear()
 
+        def permute_w1(i):
+            if i >= 2 * W1_PAIRS:
+                halves[lv_pairs[0], i % 2] = permute_half(w2_words[lv_pairs[0]], i % 2 * 2, 2 - i % 2)
+            else:
+                halves[i] = permute_half(w1_words[i // 2], i % 2 * 2, 2)
+
         for i in range(2 * W1_PAIRS):
             c, half = i // 2, i % 2
             passes = (2 * half, 2 * half + 1)
-            banks = [transpose_pass(w1_words[c], g, row0[c]) for g in passes]
-            grouped = [group_rows_even_odd(W1_COPY[g], bank) for g, bank in zip(passes, banks)]
-            if half == 1 and c + 1 < W1_PAIRS:
-                row0[c + 1] = permute_row("V", w1_words[c + 1], 0, PASSES1)
+            banks = [transpose_pass(w1_words[c], g, halves.get(i)) for g in passes]
+            grouped = [group_rows_even_odd("V" if c == 0 and g % 2 else "S", bank) for g, bank in zip(passes, banks)]
             quantise_waiting()
+            permute_w1(i + 2)
             for g, group in zip(passes, grouped):
                 waiting.append((group, w1_codes[:, c, g, :], w1_scales[:, c, g, :]))
-            if i == 0:
+            if i == 1:
                 spread_b2()
-            if i in (1, 2):
-                keep_clock_up(2)
+                keep_clock_up(1)
+            if i == 2:
+                keep_clock_up(1)
             if i in (7, 11):
                 quantise_hid(i // 4 - 1)
             if i >= 3:
@@ -233,9 +249,9 @@ def tile_vrnncell_pa_kernel(
         def cols_of(part):
             return slice(part * PAIR, (part + 1) * PAIR)
 
-        def group_w2(units):
-            banks = [transpose_pass(w2_words[q], g) for q, g in units]
-            grouped = [group_rows_in_order("S", bank) for bank in banks]
+        def group_w2(units, engines):
+            banks = [transpose_pass(w2_words[q], g, halves.get((q, g // 2))) for q, g in units]
+            grouped = [group_rows_in_order(engine, bank) for engine, bank in zip(engines, banks)]
             quantise_waiting()
             for (q, g), group in zip(units, grouped):
                 waiting.append((group, w2_codes[:, q, g, :], w2_scales[:, q, g, :]))
@@ -306,43 +322,39 @@ def tile_vrnncell_pa_kernel(
                     accum_out=kl_sum(DEV_SQ, part, t),
                 )
 
-        lv_pairs = W2_ORDER[:Z_PARTS]
-        mu_pairs = W2_ORDER[Z_PARTS:]
-
         (lv0, lv1), (mu0, mu1) = lv_pairs, mu_pairs
-        group_w2([(lv0, 0), (lv0, 1)])
+        group_w2([(lv0, 0), (lv0, 1)], "SV")
         layer1(9)
-        group_w2([(lv0, 2), (lv1, 0)])
+        group_w2([(lv0, 2), (lv1, 0)], "SV")
         layer1(10)
-        group_w2([(lv1, 1), (lv1, 2)])
         layer1(11)
-        group_w2([(mu0, 0), (mu0, 1), (mu0, 2)])
+        quantise_waiting()
         quantise_hid(PASSES2 - 1)
+        group_w2([(lv1, 1), (lv1, 2)], "SS")
         quantise_waiting()
+        group_w2([(mu0, 0), (mu0, 1)], "SV")
         lv_accs = [layer2(lv0)]
-        add_bias(lv_q, lv_accs[0], lv0, 0)
-        group_w2([(mu1, 0), (mu1, 1)])
+        group_w2([(mu0, 2)], "S")
         lv_accs.append(layer2(lv1))
-        quantise(*waiting[0])
-        clip_and_std(0)
-        quantise(*waiting[1])
-        add_bias(lv_q, lv_accs[1], lv1, 1)
-        waiting.clear()
-        group_w2([(mu1, 2)])
-        sum_lv_diff(0)
+        add_bias(lv_q, lv_accs[0], lv0, 0)
         quantise_waiting()
+        add_bias(lv_q, lv_accs[1], lv1, 1)
+        group_w2([(mu1, 0), (mu1, 1)], "SS")
+        mu_accs = [layer2(mu0)]
+        clip_and_std(0)
         clip_and_std(1)
-        sum_var_ratio(0)
-        combine(z_sb, std_q, eps_sb, ALU.mult, 0)
+        sum_lv_diff(0)
         sum_lv_diff(1)
-        sum_var_ratio(1)
-        combine(z_sb, std_q, eps_sb, ALU.mult, 1)
-
-        stats_accs = [layer2(q) for q in mu_pairs]
-        add_bias(mu_q, stats_accs[0], mu_pairs[0], 0)
+        group_w2([(mu1, 2)], "S")
+        add_bias(mu_q, mu_accs[0], mu0, 0)
         store(out_1, mu_q, 0)
+        quantise_waiting()
+        mu_accs.append(layer2(mu1))
+        sum_var_ratio(0)
+        sum_var_ratio(1)
+        combine(z_sb, std_q, eps_sb, ALU.mult, 0)
         combine(dev, mu_q, mup_sb, ALU.subtract, 0)
-        add_bias(mu_q, stats_accs[1], mu_pairs[1], 1)
+        add_bias(mu_q, mu_accs[1], mu1, 1)
         store(out_1, mu_q, 1)
         combine(dev, dev, inv_std_p, ALU.mult, 0)
         sum_dev_squares(0)
@@ -351,6 +363,7 @@ def tile_vrnncell_pa_kernel(
         store(out_0, z_sb, 0)
         combine(dev, dev, inv_std_p, ALU.mult, 1)
         sum_dev_squares(1)
+        combine(z_sb, std_q, eps_sb, ALU.mult, 1)
         combine(z_sb, z_sb, mu_q, ALU.add, 1)
         store(out_0, z_sb, 1)
 

@@ -29,8 +29,8 @@ DEV_SQ, LV_DIFF, VAR_RATIO = 0, 1, 2
 
 FLOPS = 2 * B * K1 * H + 2 * B * H * 2 * Z
 
-W1_COPY = "SSSS"
 W2_ORDER = (2, 3, 0, 1)
+
 
 def tile_vrnncell_pa_kernel(
     tc, x_t, h_prev, eps, enc_w1, enc_b1, enc_w2, enc_b2, mu_p, logvar_p, out_0, out_1, out_2, out_3
@@ -39,39 +39,35 @@ def tile_vrnncell_pa_kernel(
     with ExitStack() as ctx:
         keep = ctx.enter_context(tc.tile_pool(name="keep", bufs=1))
         stage = ctx.enter_context(tc.tile_pool(name="stage", bufs=6))
-        permuted = ctx.enter_context(tc.tile_pool(name="permuted", bufs=4))
+        sorted_rows = ctx.enter_context(tc.tile_pool(name="sorted_rows", bufs=4))
         psum_t = ctx.enter_context(tc.psum_pool(name="psum_t", bufs=6))
         psum_acc = ctx.enter_context(tc.psum_pool(name="psum_acc", bufs=2))
         ctx.enter_context(tc.manual_schedule())
 
         ones = keep.tile([P, Z], BF16)
         nc.vector.memset(ones[:], 1.0)
-        b2_row = keep.tile([P, 2 * Z], BF16)
-        nc.vector.memset(b2_row[:].bitcast(U32), 0)
         warm = keep.tile([P, 1], F32)
         nc.vector.memset(warm[:], 0.0)
         nc.scalar.activation(out=warm[:], in_=warm[:], func=ACT.Exp)
 
         def load_rows(rows, width, name, cuts=()):
-            raw = keep.tile([P, 2 * width], BF16, name=name)
+            raw = keep.tile([P, 2, width], BF16, name=name)
             edges = (0,) + cuts + (width,)
             for lo, hi in zip(edges[:-1], edges[1:]):
-                nc.sync.dma_start(out=raw[:].rearrange("p (a k) -> p a k", a=2)[:, :, lo:hi], in_=rows[:, :, lo:hi])
-            return raw[:].bitcast(F32).rearrange("p (a w) -> p a w", a=2)
+                nc.sync.dma_start(out=raw[:, :, lo:hi], in_=rows[:, :, lo:hi])
+            return raw
 
         def load_pair(rows, width, name, cuts=()):
             return load_rows(rows.rearrange("(p a) k -> p a k", a=2), width, name, cuts)
 
         def load_w1_pair(c):
             quad = enc_w1[c // 2 * K_PASS : (c // 2 + 1) * K_PASS, :].rearrange("(p t) k -> p t k", t=4)
-            return load_rows(quad[:, c % 2 * 2 : c % 2 * 2 + 2, :], K1, "w1_raw%d" % c, (K1 // 2,) if c < 2 else ())
+            cuts = (K1 // 2,) if c < 2 else ()
+            return load_rows(quad[:, c % 2 * 2 : c % 2 * 2 + 2, :], K1, "w1_raw%d" % c, cuts)
 
-        x_words = load_pair(x_t, O, "x_raw")
-        h_words = load_pair(h_prev, H, "h_raw", (K_PASS,))
-        b1_cols = keep.tile([P, PASSES2, 4], BF16)
-        nc.sync.dma_start(out=b1_cols[:], in_=enc_b1.rearrange("(g p t) -> p g t", p=P, t=4))
-        nc.sync.dma_start(out=b2_row[0:1, :], in_=enc_b2.rearrange("(o n) -> o n", o=1))
-        w1_words = [load_w1_pair(c) for c in range(W1_PAIRS)]
+        x_raw = load_pair(x_t, O, "x_raw")
+        h_raw = load_pair(h_prev, H, "h_raw", (K_PASS,))
+        w1_raw = [load_w1_pair(c) for c in range(W1_PAIRS)]
 
         def load_prior(src, name):
             prior = keep.tile([P, B_TILES, Z], BF16, name=name)
@@ -81,10 +77,15 @@ def tile_vrnncell_pa_kernel(
         lvp_sb = load_prior(logvar_p, "lvp_sb")
         mup_sb = load_prior(mu_p, "mup_sb")
         eps_sb = load_prior(eps, "eps_sb")
-        w2_words = {q: load_pair(enc_w2[q * PAIR : (q + 1) * PAIR, :], H, "w2_raw%d" % q) for q in W2_ORDER}
+        w2_raw = {q: load_pair(enc_w2[q * PAIR : (q + 1) * PAIR, :], H, "w2_raw%d" % q) for q in W2_ORDER}
 
         ident = keep.tile([P, P], F32)
         make_identity(nc, ident[:])
+        b2_row = keep.tile([P, 2 * Z], BF16)
+        nc.gpsimd.memset(b2_row[:].bitcast(U32), 0)
+        nc.gpsimd.dma_start(out=b2_row[0:1, :], in_=enc_b2.rearrange("(o n) -> o n", o=1))
+        b1_cols = keep.tile([P, PASSES2, 4], BF16)
+        nc.gpsimd.dma_start(out=b1_cols[:], in_=enc_b1.rearrange("(g p t) -> p g t", p=P, t=4))
         kl_sums = keep.tile([P, KL_TERMS * Z_PARTS, P], F32)
         nc.gpsimd.memset(kl_sums[:], 0.0)
 
@@ -99,32 +100,32 @@ def tile_vrnncell_pa_kernel(
 
         copies = {"V": nc.vector.tensor_copy, "S": nc.scalar.copy}
 
-        def permute_half(words, first, passes):
-            rows = permuted.tile([P, 2, 2, 2, P], F32, tag="rows")
+        def sort_words(raw, first, passes):
+            rows = sorted_rows.tile([P, 2, 2, passes * PAIR], BF16, tag="rows%d" % passes)
             for a in range(2):
                 nc.vector.tensor_copy(
-                    out=rows[:, a, 0:passes, :, :],
-                    in_=words[:, a, first * PAIR : (first + passes) * PAIR].rearrange(
-                        "p (g w u) -> p g u w", g=passes, u=2
-                    ),
+                    out=rows[:, a, :, :].rearrange("p u (x w) -> p u x w", w=16),
+                    in_=raw[:, a, first * K_PASS : (first + passes) * K_PASS].rearrange("p (x u w) -> p u x w", u=2, w=16),
                 )
-            return rows
+            return [rows[:, :, :, g * PAIR : (g + 1) * PAIR] for g in range(passes)]
 
-        def transpose_pass(words, g, rows=None):
-            bank = psum_t.tile([P, 4 * P], F32)
+        def transpose_rows(word_source):
+            bank = psum_t.tile([P, 4 * P], F32, tag="bank")
             for a in range(2):
                 for u in range(2):
-                    if rows is None:
-                        in_ap = words[:, a, 2 * g * P + u : 2 * (g + 1) * P : 2]
-                    else:
-                        in_ap = rows[:, a, g % 2, u, :]
                     nc.tensor.transpose(
-                        out=bank[:, (2 * a + u) * P : (2 * a + u + 1) * P], in_=in_ap, identity=ident[:]
+                        out=bank[:, (2 * a + u) * P : (2 * a + u + 1) * P], in_=word_source(a, u), identity=ident[:]
                     )
             return bank
 
+        def transpose_sorted(rows):
+            return transpose_rows(lambda a, u: rows[:, a, u, :].bitcast(F32))
+
+        def transpose_strided(raw, g):
+            return transpose_rows(lambda a, u: raw[:, a, g * K_PASS : (g + 1) * K_PASS].bitcast(F32)[:, u::2])
+
         def group_rows_in_order(engine, bank):
-            grouped = stage.tile([P, 4 * PAIR], BF16, align_bytes=64)
+            grouped = stage.tile([P, 4 * PAIR], BF16, align_bytes=64, tag="grouped")
             copies[engine](
                 out=grouped[:].bitcast(F32).rearrange("p (r a u) -> p r a u", a=2, u=2),
                 in_=bank[:].rearrange("p (a u r) -> p r a u", a=2, u=2),
@@ -132,7 +133,7 @@ def tile_vrnncell_pa_kernel(
             return grouped
 
         def group_rows_even_odd(engine, bank):
-            grouped = stage.tile([P, 4 * PAIR], BF16, align_bytes=64)
+            grouped = stage.tile([P, 4 * PAIR], BF16, align_bytes=64, tag="grouped")
             copies[engine](
                 out=grouped[:].bitcast(F32).rearrange("p (a r u) -> p a r u", a=2, u=2),
                 in_=bank[:].rearrange("p (a u r) -> p a r u", a=2, u=2),
@@ -147,12 +148,6 @@ def tile_vrnncell_pa_kernel(
                 unread = psum_acc.tile([P, Z], F32, tag="acc")
                 nc.tensor.matmul(out=unread[:], lhsT=ones[:, 0:P], rhs=ones[:], start=True, stop=True)
 
-        keep_clock_up(4)
-        x_banks = [transpose_pass(x_words, 0)] + [transpose_pass(h_words, g) for g in range(PASSES1 - 1)]
-        x_grouped = [group_rows_in_order("VS"[g % 2], x_banks[g]) for g in range(PASSES1)]
-        for g in range(PASSES1):
-            quantise(x_grouped[g], x_codes[:, g, :], x_scales[:, g, :])
-
         b2_all = keep.tile([P, 2 * Z], F32)
 
         def spread_b2():
@@ -161,7 +156,17 @@ def tile_vrnncell_pa_kernel(
                 nc.tensor.matmul(
                     out=b2_bank[:], lhsT=ones[:, 0:P], rhs=b2_row[:, half * Z : (half + 1) * Z], start=True, stop=True
                 )
-                nc.scalar.copy(out=b2_all[:, half * Z : (half + 1) * Z], in_=b2_bank[:])
+                copies["S"](out=b2_all[:, half * Z : (half + 1) * Z], in_=b2_bank[:])
+
+        keep_clock_up(3)
+        x_rows = sort_words(x_raw, 0, 1) + sort_words(h_raw, 0, 1) + sort_words(h_raw, 1, 2)
+        x_banks = [transpose_sorted(rows) for rows in x_rows]
+        sorted_halves = {0: sort_words(w1_raw[0], 0, 2)}
+        x_grouped = [group_rows_in_order("VSVS"[g], x_banks[g]) for g in range(PASSES1)]
+        sorted_halves[1] = sort_words(w1_raw[0], 2, 2)
+        for g in range(PASSES1):
+            quantise(x_grouped[g], x_codes[:, g, :], x_scales[:, g, :])
+        spread_b2()
 
         hid_rows = keep.tile([P, 2 * W1_PAIRS, B], BF16)
         inv_std_p = keep.tile([P, B_TILES, Z], F32)
@@ -197,9 +202,6 @@ def tile_vrnncell_pa_kernel(
                     in_=hid_grouped[:, bt, :, :].rearrange("p b t -> p (b t)"),
                 )
 
-        lv_pairs = W2_ORDER[:Z_PARTS]
-        mu_pairs = W2_ORDER[Z_PARTS:]
-        halves = {}
         waiting = []
 
         def quantise_waiting():
@@ -207,32 +209,23 @@ def tile_vrnncell_pa_kernel(
                 quantise(*args)
             waiting.clear()
 
-        def permute_w1(i):
-            if i >= 2 * W1_PAIRS:
-                halves[lv_pairs[0], i % 2] = permute_half(w2_words[lv_pairs[0]], i % 2 * 2, 2 - i % 2)
-            else:
-                halves[i] = permute_half(w1_words[i // 2], i % 2 * 2, 2)
-
         for i in range(2 * W1_PAIRS):
             c, half = i // 2, i % 2
-            passes = (2 * half, 2 * half + 1)
-            banks = [transpose_pass(w1_words[c], g, halves.get(i)) for g in passes]
-            grouped = [group_rows_even_odd("V" if c == 0 and g % 2 else "S", bank) for g, bank in zip(passes, banks)]
+            banks = [transpose_sorted(rows) for rows in sorted_halves[i]]
+            grouped = [group_rows_even_odd("SSSS"[2 * half + g], banks[g]) for g in range(2)]
             quantise_waiting()
-            permute_w1(i + 2)
-            for g, group in zip(passes, grouped):
-                waiting.append((group, w1_codes[:, c, g, :], w1_scales[:, c, g, :]))
+            if i + 2 < 2 * W1_PAIRS:
+                sorted_halves[i + 2] = sort_words(w1_raw[(i + 2) // 2], i % 2 * 2, 2)
+            for g in range(2):
+                waiting.append((grouped[g], w1_codes[:, c, 2 * half + g, :], w1_scales[:, c, 2 * half + g, :]))
             if i == 1:
-                spread_b2()
-                keep_clock_up(1)
+                keep_clock_up(2)
             if i == 2:
-                keep_clock_up(1)
+                keep_clock_up(2)
             if i in (7, 11):
                 quantise_hid(i // 4 - 1)
             if i >= 3:
                 layer1(i - 3)
-            if i == 8:
-                nc.scalar.activation(out=inv_std_p[:], in_=lvp_sb[:], func=ACT.Exp, scale=-0.5)
 
         mu_q = keep.tile([P, B_TILES, Z], F32)
         lv_q = keep.tile([P, B_TILES, Z], F32)
@@ -250,7 +243,7 @@ def tile_vrnncell_pa_kernel(
             return slice(part * PAIR, (part + 1) * PAIR)
 
         def group_w2(units, engines):
-            banks = [transpose_pass(w2_words[q], g, halves.get((q, g // 2))) for q, g in units]
+            banks = [transpose_strided(w2_raw[q], g) for q, g in units]
             grouped = [group_rows_in_order(engine, bank) for engine, bank in zip(engines, banks)]
             quantise_waiting()
             for (q, g), group in zip(units, grouped):
@@ -322,17 +315,18 @@ def tile_vrnncell_pa_kernel(
                     accum_out=kl_sum(DEV_SQ, part, t),
                 )
 
-        (lv0, lv1), (mu0, mu1) = lv_pairs, mu_pairs
-        group_w2([(lv0, 0), (lv0, 1)], "SV")
+        (lv0, lv1), (mu0, mu1) = W2_ORDER[:Z_PARTS], W2_ORDER[Z_PARTS:]
+        group_w2([(lv0, 0), (lv0, 1)], "SS")
         layer1(9)
-        group_w2([(lv0, 2), (lv1, 0)], "SV")
+        group_w2([(lv0, 2), (lv1, 0)], "SS")
         layer1(10)
         layer1(11)
         quantise_waiting()
         quantise_hid(PASSES2 - 1)
         group_w2([(lv1, 1), (lv1, 2)], "SS")
         quantise_waiting()
-        group_w2([(mu0, 0), (mu0, 1)], "SV")
+        group_w2([(mu0, 0), (mu0, 1)], "SS")
+        nc.scalar.activation(out=inv_std_p[:], in_=lvp_sb[:], func=ACT.Exp, scale=-0.5)
         lv_accs = [layer2(lv0)]
         group_w2([(mu0, 2)], "S")
         lv_accs.append(layer2(lv1))

@@ -46,6 +46,11 @@ def tile_vrnncell_pa_kernel(
 
         ones = keep.tile([P, Z], BF16)
         nc.vector.memset(ones[:], 1.0)
+        b1_cols = keep.tile([P, PASSES2, 4], BF16)
+        nc.scalar.dma_start(out=b1_cols[:], in_=enc_b1.rearrange("(g p t) -> p g t", p=P, t=4))
+        b2_row = keep.tile([P, 2 * Z], BF16)
+        nc.vector.memset(b2_row[:].bitcast(U32), 0)
+        nc.scalar.dma_start(out=b2_row[0:1, :], in_=enc_b2.rearrange("(o n) -> o n", o=1))
         warm = keep.tile([P, 1], F32)
         nc.vector.memset(warm[:], 0.0)
         nc.scalar.activation(out=warm[:], in_=warm[:], func=ACT.Exp)
@@ -81,11 +86,8 @@ def tile_vrnncell_pa_kernel(
 
         ident = keep.tile([P, P], F32)
         make_identity(nc, ident[:])
-        b2_row = keep.tile([P, 2 * Z], BF16)
-        nc.gpsimd.memset(b2_row[:].bitcast(U32), 0)
-        nc.gpsimd.dma_start(out=b2_row[0:1, :], in_=enc_b2.rearrange("(o n) -> o n", o=1))
-        b1_cols = keep.tile([P, PASSES2, 4], BF16)
-        nc.gpsimd.dma_start(out=b1_cols[:], in_=enc_b1.rearrange("(g p t) -> p g t", p=P, t=4))
+        neg_ident = keep.tile([P, P], BF16)
+        nc.gpsimd.tensor_scalar(out=neg_ident[:], in0=ident[:], scalar1=-1.0, scalar2=None, op0=ALU.mult)
         kl_sums = keep.tile([P, KL_TERMS * Z_PARTS, P], F32)
         nc.gpsimd.memset(kl_sums[:], 0.0)
 
@@ -162,11 +164,10 @@ def tile_vrnncell_pa_kernel(
         x_rows = sort_words(x_raw, 0, 1) + sort_words(h_raw, 0, 1) + sort_words(h_raw, 1, 2)
         x_banks = [transpose_sorted(rows) for rows in x_rows]
         sorted_halves = {0: sort_words(w1_raw[0], 0, 2)}
-        x_grouped = [group_rows_in_order("VSVS"[g], x_banks[g]) for g in range(PASSES1)]
+        x_grouped = [group_rows_in_order("SSSS"[g], x_banks[g]) for g in range(PASSES1)]
         sorted_halves[1] = sort_words(w1_raw[0], 2, 2)
         for g in range(PASSES1):
             quantise(x_grouped[g], x_codes[:, g, :], x_scales[:, g, :])
-        spread_b2()
 
         hid_rows = keep.tile([P, 2 * W1_PAIRS, B], BF16)
         inv_std_p = keep.tile([P, B_TILES, Z], F32)
@@ -219,20 +220,23 @@ def tile_vrnncell_pa_kernel(
             for g in range(2):
                 waiting.append((grouped[g], w1_codes[:, c, 2 * half + g, :], w1_scales[:, c, 2 * half + g, :]))
             if i == 1:
-                keep_clock_up(2)
+                keep_clock_up(1)
             if i == 2:
-                keep_clock_up(2)
+                keep_clock_up(1)
+            if i == 0:
+                spread_b2()
             if i in (7, 11):
                 quantise_hid(i // 4 - 1)
-            if i >= 3:
-                layer1(i - 3)
+            if half == 1 and c > 0:
+                layer1(2 * c - 2)
+                layer1(2 * c - 1)
 
         mu_q = keep.tile([P, B_TILES, Z], F32)
         lv_q = keep.tile([P, B_TILES, Z], F32)
         std_q = keep.tile([P, B_TILES, Z], F32)
         z_sb = keep.tile([P, B_TILES, Z], F32)
         dev = keep.tile([P, B_TILES, Z], F32)
-        lv_diff = keep.tile([P, B_TILES, Z], F32)
+        lv_diff = keep.tile([P, B_TILES, Z], BF16)
         dev_sq = keep.tile([P, B_TILES, Z], BF16)
         var_ratio = keep.tile([P, B_TILES, Z], BF16)
 
@@ -284,25 +288,26 @@ def tile_vrnncell_pa_kernel(
             store(out_2, lv_q, part)
             nc.scalar.activation(out=std_q[:, :, cols], in_=lv_q[:, :, cols], func=ACT.Exp, scale=0.5)
 
-        def sum_lv_diff(part):
+        def lv_diff_bank(part):
+            bank = psum_t.tile([P, B_TILES, PAIR], F32, tag="bank")
             for t in range(B_TILES):
-                nc.vector.scalar_tensor_tensor(
-                    out=lv_diff[:, t, cols_of(part)],
-                    in0=lv_q[:, t, cols_of(part)],
-                    scalar=-1.0,
-                    in1=lvp_sb[:, t, cols_of(part)],
-                    op0=ALU.mult,
-                    op1=ALU.add,
-                    accum_out=kl_sum(LV_DIFF, part, t),
-                )
+                nc.tensor.matmul(out=bank[:, t, :], lhsT=neg_ident[:], rhs=lvp_sb[:, t, cols_of(part)], start=True, stop=False)
+                nc.tensor.matmul(out=bank[:, t, :], lhsT=ident[:], rhs=lv_q[:, t, cols_of(part)], start=False, stop=True)
+            return bank
 
-        def sum_var_ratio(part):
+        def sum_var_ratio(part, bank):
             for t in range(B_TILES):
                 nc.scalar.activation(
-                    out=var_ratio[:, t, cols_of(part)],
-                    in_=lv_diff[:, t, cols_of(part)],
-                    func=ACT.Exp,
+                    out=lv_diff[:, t, cols_of(part)],
+                    in_=bank[:, t, :],
+                    func=ACT.Identity,
                     scale=-1.0,
+                    accum_out=kl_sum(LV_DIFF, part, t),
+                )
+                nc.scalar.activation(
+                    out=var_ratio[:, t, cols_of(part)],
+                    in_=bank[:, t, :],
+                    func=ACT.Exp,
                     accum_out=kl_sum(VAR_RATIO, part, t),
                 )
 
@@ -317,7 +322,6 @@ def tile_vrnncell_pa_kernel(
 
         (lv0, lv1), (mu0, mu1) = W2_ORDER[:Z_PARTS], W2_ORDER[Z_PARTS:]
         group_w2([(lv0, 0), (lv0, 1)], "SS")
-        layer1(9)
         group_w2([(lv0, 2), (lv1, 0)], "SS")
         layer1(10)
         layer1(11)
@@ -328,24 +332,23 @@ def tile_vrnncell_pa_kernel(
         group_w2([(mu0, 0), (mu0, 1)], "SS")
         nc.scalar.activation(out=inv_std_p[:], in_=lvp_sb[:], func=ACT.Exp, scale=-0.5)
         lv_accs = [layer2(lv0)]
-        group_w2([(mu0, 2)], "S")
-        lv_accs.append(layer2(lv1))
+        group_w2([(mu0, 2), (mu1, 0)], "SS")
         add_bias(lv_q, lv_accs[0], lv0, 0)
+        lv_accs.append(layer2(lv1))
         quantise_waiting()
+        group_w2([(mu1, 1), (mu1, 2)], "SS")
         add_bias(lv_q, lv_accs[1], lv1, 1)
-        group_w2([(mu1, 0), (mu1, 1)], "SS")
-        mu_accs = [layer2(mu0)]
         clip_and_std(0)
+        mu_accs = [layer2(mu0)]
+        quantise_waiting()
         clip_and_std(1)
-        sum_lv_diff(0)
-        sum_lv_diff(1)
-        group_w2([(mu1, 2)], "S")
+        diff_banks = [lv_diff_bank(0)]
         add_bias(mu_q, mu_accs[0], mu0, 0)
         store(out_1, mu_q, 0)
-        quantise_waiting()
         mu_accs.append(layer2(mu1))
-        sum_var_ratio(0)
-        sum_var_ratio(1)
+        diff_banks.append(lv_diff_bank(1))
+        sum_var_ratio(0, diff_banks[0])
+        sum_var_ratio(1, diff_banks[1])
         combine(z_sb, std_q, eps_sb, ALU.mult, 0)
         combine(dev, mu_q, mup_sb, ALU.subtract, 0)
         add_bias(mu_q, mu_accs[1], mu1, 1)

@@ -63,7 +63,7 @@ def tile_vrnncell_pa_kernel(
             return raw
 
         def load_pair(rows, width, name, cuts=()):
-            return load_rows(rows.rearrange("(p a) k -> p a k", a=2), width, name, cuts)
+            return load_rows(rows.rearrange("(a p) k -> p a k", a=2), width, name, cuts)
 
         def load_w1_pair(c):
             quad = enc_w1[c // 2 * K_PASS : (c // 2 + 1) * K_PASS, :].rearrange("(p t) k -> p t k", t=4)
@@ -126,15 +126,7 @@ def tile_vrnncell_pa_kernel(
         def transpose_strided(raw, g):
             return transpose_rows(lambda a, u: raw[:, a, g * K_PASS : (g + 1) * K_PASS].bitcast(F32)[:, u::2])
 
-        def group_rows_in_order(engine, bank):
-            grouped = stage.tile([P, 4 * PAIR], BF16, align_bytes=64, tag="grouped")
-            copies[engine](
-                out=grouped[:].bitcast(F32).rearrange("p (r a u) -> p r a u", a=2, u=2),
-                in_=bank[:].rearrange("p (a u r) -> p r a u", a=2, u=2),
-            )
-            return grouped
-
-        def group_rows_even_odd(engine, bank):
+        def group_rows(engine, bank):
             grouped = stage.tile([P, 4 * PAIR], BF16, align_bytes=64, tag="grouped")
             copies[engine](
                 out=grouped[:].bitcast(F32).rearrange("p (a r u) -> p a r u", a=2, u=2),
@@ -164,7 +156,7 @@ def tile_vrnncell_pa_kernel(
         x_rows = sort_words(x_raw, 0, 1) + sort_words(h_raw, 0, 1) + sort_words(h_raw, 1, 2)
         x_banks = [transpose_sorted(rows) for rows in x_rows]
         sorted_halves = {0: sort_words(w1_raw[0], 0, 2)}
-        x_grouped = [group_rows_in_order("SSSS"[g], x_banks[g]) for g in range(PASSES1)]
+        x_grouped = [group_rows("SSSS"[g], x_banks[g]) for g in range(PASSES1)]
         sorted_halves[1] = sort_words(w1_raw[0], 2, 2)
         for g in range(PASSES1):
             quantise(x_grouped[g], x_codes[:, g, :], x_scales[:, g, :])
@@ -213,7 +205,7 @@ def tile_vrnncell_pa_kernel(
         for i in range(2 * W1_PAIRS):
             c, half = i // 2, i % 2
             banks = [transpose_sorted(rows) for rows in sorted_halves[i]]
-            grouped = [group_rows_even_odd("SSSS"[2 * half + g], banks[g]) for g in range(2)]
+            grouped = [group_rows("SSSS"[2 * half + g], banks[g]) for g in range(2)]
             quantise_waiting()
             if i + 2 < 2 * W1_PAIRS:
                 sorted_halves[i + 2] = sort_words(w1_raw[(i + 2) // 2], i % 2 * 2, 2)
@@ -248,7 +240,7 @@ def tile_vrnncell_pa_kernel(
 
         def group_w2(units, engines):
             banks = [transpose_strided(w2_raw[q], g) for q, g in units]
-            grouped = [group_rows_in_order(engine, bank) for engine, bank in zip(engines, banks)]
+            grouped = [group_rows(engine, bank) for engine, bank in zip(engines, banks)]
             quantise_waiting()
             for (q, g), group in zip(units, grouped):
                 waiting.append((group, w2_codes[:, q, g, :], w2_scales[:, q, g, :]))
@@ -312,7 +304,15 @@ def tile_vrnncell_pa_kernel(
                 )
 
         def sum_dev_squares(part):
+            cols = cols_of(part)
             for t in range(B_TILES):
+                nc.vector.tensor_tensor(
+                    out=dev[:, t, cols], in0=mu_q[:, t, cols], in1=mup_sb[:, t, cols], op=ALU.subtract
+                )
+            for t in range(B_TILES):
+                nc.vector.tensor_tensor(
+                    out=dev[:, t, cols], in0=dev[:, t, cols], in1=inv_std_p[:, t, cols], op=ALU.mult
+                )
                 nc.scalar.activation(
                     out=dev_sq[:, t, cols_of(part)],
                     in_=dev[:, t, cols_of(part)],
@@ -348,19 +348,15 @@ def tile_vrnncell_pa_kernel(
         mu_accs.append(layer2(mu1))
         diff_banks.append(lv_diff_bank(1))
         sum_var_ratio(0, diff_banks[0])
-        sum_var_ratio(1, diff_banks[1])
         combine(z_sb, std_q, eps_sb, ALU.mult, 0)
-        combine(dev, mu_q, mup_sb, ALU.subtract, 0)
+        sum_dev_squares(0)
         add_bias(mu_q, mu_accs[1], mu1, 1)
         store(out_1, mu_q, 1)
-        combine(dev, dev, inv_std_p, ALU.mult, 0)
-        sum_dev_squares(0)
-        combine(dev, mu_q, mup_sb, ALU.subtract, 1)
+        sum_var_ratio(1, diff_banks[1])
+        combine(z_sb, std_q, eps_sb, ALU.mult, 1)
+        sum_dev_squares(1)
         combine(z_sb, z_sb, mu_q, ALU.add, 0)
         store(out_0, z_sb, 0)
-        combine(dev, dev, inv_std_p, ALU.mult, 1)
-        sum_dev_squares(1)
-        combine(z_sb, std_q, eps_sb, ALU.mult, 1)
         combine(z_sb, z_sb, mu_q, ALU.add, 1)
         store(out_0, z_sb, 1)
 

from contextlib import ExitStack

import concourse.mybir as mybir
from concourse.masks import make_identity

F32 = mybir.dt.float32
BF16 = mybir.dt.bfloat16
U32 = mybir.dt.uint32
U8 = mybir.dt.uint8
FP8X4 = mybir.dt.float8_e4m3fn_x4
ACT = mybir.ActivationFunctionType
ALU = mybir.AluOpType

P = 128
K_PASS = 4 * P
PAIR = 2 * P

B, O, H, Z = 256, 512, 1536, 512
K1 = O + H
PASSES1 = K1 // K_PASS
PASSES2 = H // K_PASS
W1_PAIRS = H // PAIR
W2_PAIRS = 2 * Z // PAIR
B_TILES = B // P
Z_PARTS = Z // PAIR
CLAMP = 10.0
KL_TERMS = 3
DEV_SQ, LV_DIFF, VAR_RATIO = 0, 1, 2

FLOPS = 2 * B * K1 * H + 2 * B * H * 2 * Z

W2_ORDER = (2, 3, 0, 1)


def tile_vrnncell_pa_kernel(
    tc, x_t, h_prev, eps, enc_w1, enc_b1, enc_w2, enc_b2, mu_p, logvar_p, out_0, out_1, out_2, out_3
):
    nc = tc.nc
    with ExitStack() as ctx:
        keep = ctx.enter_context(tc.tile_pool(name="keep", bufs=1))
        stage = ctx.enter_context(tc.tile_pool(name="stage", bufs=6))
        sorted_rows = ctx.enter_context(tc.tile_pool(name="sorted_rows", bufs=4))
        psum_t = ctx.enter_context(tc.psum_pool(name="psum_t", bufs=6))
        psum_acc = ctx.enter_context(tc.psum_pool(name="psum_acc", bufs=2))
        ctx.enter_context(tc.manual_schedule())

        ones = keep.tile([P, Z], BF16)
        nc.vector.memset(ones[:], 1.0)
        b1_cols = keep.tile([P, PASSES2, 4], BF16)
        nc.scalar.dma_start(out=b1_cols[:], in_=enc_b1.rearrange("(g p t) -> p g t", p=P, t=4))
        b2_row = keep.tile([P, 2 * Z], BF16)
        nc.vector.memset(b2_row[:].bitcast(U32), 0)
        nc.scalar.dma_start(out=b2_row[0:1, :], in_=enc_b2.rearrange("(o n) -> o n", o=1))
        warm = keep.tile([P, 1], F32)
        nc.vector.memset(warm[:], 0.0)
        nc.scalar.activation(out=warm[:], in_=warm[:], func=ACT.Exp)

        def load_rows(rows, width, name, cuts=()):
            raw = keep.tile([P, 2, width], BF16, name=name)
            edges = (0,) + cuts + (width,)
            for lo, hi in zip(edges[:-1], edges[1:]):
                nc.sync.dma_start(out=raw[:, :, lo:hi], in_=rows[:, :, lo:hi])
            return raw

        def load_pair(rows, width, name, cuts=()):
            return load_rows(rows.rearrange("(a p) k -> p a k", a=2), width, name, cuts)

        def load_w1_pair(c):
            quad = enc_w1[c // 2 * K_PASS : (c // 2 + 1) * K_PASS, :].rearrange("(p t) k -> p t k", t=4)
            cuts = (K1 // 2,) if c < 2 else ()
            return load_rows(quad[:, c % 2 * 2 : c % 2 * 2 + 2, :], K1, "w1_raw%d" % c, cuts)

        x_raw = load_pair(x_t, O, "x_raw")
        h_raw = load_pair(h_prev, H, "h_raw", (K_PASS,))
        w1_raw = [load_w1_pair(c) for c in range(W1_PAIRS)]

        def load_prior(src, name):
            prior = keep.tile([P, B_TILES, Z], BF16, name=name)
            nc.sync.dma_start(out=prior[:], in_=src.rearrange("(t p) z -> p t z", p=P))
            return prior

        lvp_sb = load_prior(logvar_p, "lvp_sb")
        mup_sb = load_prior(mu_p, "mup_sb")
        eps_sb = load_prior(eps, "eps_sb")
        w2_raw = {q: load_pair(enc_w2[q * PAIR : (q + 1) * PAIR, :], H, "w2_raw%d" % q) for q in W2_ORDER}

        ident = keep.tile([P, P], F32)
        make_identity(nc, ident[:])
        neg_ident = keep.tile([P, P], BF16)
        nc.gpsimd.tensor_scalar(out=neg_ident[:], in0=ident[:], scalar1=-1.0, scalar2=None, op0=ALU.mult)
        kl_sums = keep.tile([P, KL_TERMS * Z_PARTS, P], F32)
        nc.gpsimd.memset(kl_sums[:], 0.0)

        x_codes = keep.tile([P, PASSES1, B], U32, align_bytes=64)
        x_scales = keep.tile([P, PASSES1, B], U8, align_bytes=64)
        w1_codes = keep.tile([P, W1_PAIRS, PASSES1, PAIR], U32, align_bytes=64)
        w1_scales = keep.tile([P, W1_PAIRS, PASSES1, PAIR], U8, align_bytes=64)
        hid_codes = keep.tile([P, PASSES2, B], U32, align_bytes=64)
        hid_scales = keep.tile([P, PASSES2, B], U8, align_bytes=64)
        w2_codes = keep.tile([P, W2_PAIRS, PASSES2, PAIR], U32, align_bytes=64)
        w2_scales = keep.tile([P, W2_PAIRS, PASSES2, PAIR], U8, align_bytes=64)

        copies = {"V": nc.vector.tensor_copy, "S": nc.scalar.copy}

        def sort_words(raw, first, passes):
            rows = sorted_rows.tile([P, 2, 2, passes * PAIR], BF16, tag="rows%d" % passes)
            for a in range(2):
                nc.vector.tensor_copy(
                    out=rows[:, a, :, :].rearrange("p u (x w) -> p u x w", w=16),
                    in_=raw[:, a, first * K_PASS : (first + passes) * K_PASS].rearrange("p (x u w) -> p u x w", u=2, w=16),
                )
            return [rows[:, :, :, g * PAIR : (g + 1) * PAIR] for g in range(passes)]

        def transpose_rows(word_source):
            bank = psum_t.tile([P, 4 * P], F32, tag="bank")
            for a in range(2):
                for u in range(2):
                    nc.tensor.transpose(
                        out=bank[:, (2 * a + u) * P : (2 * a + u + 1) * P], in_=word_source(a, u), identity=ident[:]
                    )
            return bank

        def transpose_sorted(rows):
            return transpose_rows(lambda a, u: rows[:, a, u, :].bitcast(F32))

        def transpose_strided(raw, g):
            return transpose_rows(lambda a, u: raw[:, a, g * K_PASS : (g + 1) * K_PASS].bitcast(F32)[:, u::2])

        def group_rows(engine, bank):
            grouped = stage.tile([P, 4 * PAIR], BF16, align_bytes=64, tag="grouped")
            copies[engine](
                out=grouped[:].bitcast(F32).rearrange("p (a r u) -> p a r u", a=2, u=2),
                in_=bank[:].rearrange("p (a u r) -> p a r u", a=2, u=2),
            )
            return grouped

        def quantise(grouped, codes, scales):
            nc.vector.quantize_mx(out=codes.bitcast(FP8X4), scales=scales, in_=grouped[:])

        def keep_clock_up(count):
            for n in range(count):
                unread = psum_acc.tile([P, Z], F32, tag="acc")
                nc.tensor.matmul(out=unread[:], lhsT=ones[:, 0:P], rhs=ones[:], start=True, stop=True)

        b2_all = keep.tile([P, 2 * Z], F32)

        def spread_b2():
            for half in range(2):
                b2_bank = psum_acc.tile([P, Z], F32, tag="acc")
                nc.tensor.matmul(
                    out=b2_bank[:], lhsT=ones[:, 0:P], rhs=b2_row[:, half * Z : (half + 1) * Z], start=True, stop=True
                )
                copies["S"](out=b2_all[:, half * Z : (half + 1) * Z], in_=b2_bank[:])

        keep_clock_up(3)
        x_rows = sort_words(x_raw, 0, 1) + sort_words(h_raw, 0, 1) + sort_words(h_raw, 1, 2)
        x_banks = [transpose_sorted(rows) for rows in x_rows]
        sorted_halves = {0: sort_words(w1_raw[0], 0, 2)}
        x_grouped = [group_rows("SSSS"[g], x_banks[g]) for g in range(PASSES1)]
        sorted_halves[1] = sort_words(w1_raw[0], 2, 2)
        for g in range(PASSES1):
            quantise(x_grouped[g], x_codes[:, g, :], x_scales[:, g, :])

        hid_rows = keep.tile([P, 2 * W1_PAIRS, B], BF16)
        inv_std_p = keep.tile([P, B_TILES, Z], F32)

        def layer1(m):
            c, e = m // 2, m % 2
            hid_acc = psum_acc.tile([P, B], F32, tag="acc")
            for g in range(PASSES1):
                nc.tensor.matmul_mx(
                    out=hid_acc[:],
                    lhsT=w1_codes[:, c, g, e * P : (e + 1) * P].bitcast(FP8X4),
                    lhsT_scale=w1_scales[:, c, g, e * P : (e + 1) * P],
                    rhs=x_codes[:, g, :].bitcast(FP8X4),
                    rhs_scale=x_scales[:, g, :],
                    start=(g == 0),
                    stop=(g == PASSES1 - 1),
                )
            nc.scalar.activation(
                out=hid_rows[:, m, :], in_=hid_acc[:], func=ACT.Relu, bias=b1_cols[:, m // 4, m % 4 : m % 4 + 1]
            )

        def quantise_hid(g):
            hid_grouped = stage.tile([P, B_TILES, P, 4], BF16, align_bytes=64, tag="grouped")
            for bt in range(B_TILES):
                nc.vector.tensor_copy(
                    out=hid_grouped[:, bt, :, :],
                    in_=hid_rows[:, 4 * g : 4 * g + 4, bt * P : (bt + 1) * P].rearrange("p t b -> p b t"),
                )
            for bt in range(B_TILES):
                nc.vector.quantize_mx(
                    out=hid_codes[:, g, bt * P : (bt + 1) * P].bitcast(FP8X4),
                    scales=hid_scales[:, g, bt * P : (bt + 1) * P],
                    in_=hid_grouped[:, bt, :, :].rearrange("p b t -> p (b t)"),
                )

        waiting = []

        def quantise_waiting():
            for args in waiting:
                quantise(*args)
            waiting.clear()

        for i in range(2 * W1_PAIRS):
            c, half = i // 2, i % 2
            banks = [transpose_sorted(rows) for rows in sorted_halves[i]]
            grouped = [group_rows("SSSS"[2 * half + g], banks[g]) for g in range(2)]
            quantise_waiting()
            if i + 2 < 2 * W1_PAIRS:
                sorted_halves[i + 2] = sort_words(w1_raw[(i + 2) // 2], i % 2 * 2, 2)
            for g in range(2):
                waiting.append((grouped[g], w1_codes[:, c, 2 * half + g, :], w1_scales[:, c, 2 * half + g, :]))
            if i == 1:
                keep_clock_up(1)
            if i == 2:
                keep_clock_up(1)
            if i == 0:
                spread_b2()
            if i in (7, 11):
                quantise_hid(i // 4 - 1)
            if half == 1 and c > 0:
                layer1(2 * c - 2)
                layer1(2 * c - 1)

        mu_q = keep.tile([P, B_TILES, Z], F32)
        lv_q = keep.tile([P, B_TILES, Z], F32)
        std_q = keep.tile([P, B_TILES, Z], F32)
        z_sb = keep.tile([P, B_TILES, Z], F32)
        dev = keep.tile([P, B_TILES, Z], F32)
        lv_diff = keep.tile([P, B_TILES, Z], BF16)
        dev_sq = keep.tile([P, B_TILES, Z], BF16)
        var_ratio = keep.tile([P, B_TILES, Z], BF16)

        def kl_sum(term, part, t):
            return kl_sums[:, term * Z_PARTS + part, t : t + 1]

        def cols_of(part):
            return slice(part * PAIR, (part + 1) * PAIR)

        def group_w2(units, engines):
            banks = [transpose_strided(w2_raw[q], g) for q, g in units]
            grouped = [group_rows(engine, bank) for engine, bank in zip(engines, banks)]
            quantise_waiting()
            for (q, g), group in zip(units, grouped):
                waiting.append((group, w2_codes[:, q, g, :], w2_scales[:, q, g, :]))

        def layer2(q):
            stats_acc = psum_acc.tile([P, B_TILES, PAIR], F32, tag="acc")
            for t in range(B_TILES):
                for g in range(PASSES2):
                    nc.tensor.matmul_mx(
                        out=stats_acc[:, t, :],
                        lhsT=hid_codes[:, g, t * P : (t + 1) * P].bitcast(FP8X4),
                        lhsT_scale=hid_scales[:, g, t * P : (t + 1) * P],
                        rhs=w2_codes[:, q, g, :].bitcast(FP8X4),
                        rhs_scale=w2_scales[:, q, g, :],
                        start=(g == 0),
                        stop=(g == PASSES2 - 1),
                    )
            return stats_acc

        def add_bias(out, stats_acc, q, part):
            bias = b2_all[:, q * PAIR : (q + 1) * PAIR].unsqueeze(1).to_broadcast([P, B_TILES, PAIR])
            nc.vector.tensor_tensor(out=out[:, :, cols_of(part)], in0=stats_acc[:], in1=bias, op=ALU.add)

        def store(out, tile, part):
            cols = cols_of(part)
            nc.sync.dma_start(out=out.rearrange("(t p) z -> p t z", p=P)[:, :, cols], in_=tile[:, :, cols])

        def combine(out, in0, in1, op, part):
            cols = cols_of(part)
            nc.vector.tensor_tensor(out=out[:, :, cols], in0=in0[:, :, cols], in1=in1[:, :, cols], op=op)

        def clip_and_std(part):
            cols = cols_of(part)
            nc.vector.tensor_scalar(
                out=lv_q[:, :, cols], in0=lv_q[:, :, cols], scalar1=CLAMP, scalar2=-CLAMP, op0=ALU.min, op1=ALU.max
            )
            store(out_2, lv_q, part)
            nc.scalar.activation(out=std_q[:, :, cols], in_=lv_q[:, :, cols], func=ACT.Exp, scale=0.5)

        def lv_diff_bank(part):
            bank = psum_t.tile([P, B_TILES, PAIR], F32, tag="bank")
            for t in range(B_TILES):
                nc.tensor.matmul(out=bank[:, t, :], lhsT=neg_ident[:], rhs=lvp_sb[:, t, cols_of(part)], start=True, stop=False)
                nc.tensor.matmul(out=bank[:, t, :], lhsT=ident[:], rhs=lv_q[:, t, cols_of(part)], start=False, stop=True)
            return bank

        def sum_var_ratio(part, bank):
            for t in range(B_TILES):
                nc.scalar.activation(
                    out=lv_diff[:, t, cols_of(part)],
                    in_=bank[:, t, :],
                    func=ACT.Identity,
                    scale=-1.0,
                    accum_out=kl_sum(LV_DIFF, part, t),
                )
                nc.scalar.activation(
                    out=var_ratio[:, t, cols_of(part)],
                    in_=bank[:, t, :],
                    func=ACT.Exp,
                    accum_out=kl_sum(VAR_RATIO, part, t),
                )

        def sum_dev_squares(part):
            cols = cols_of(part)
            for t in range(B_TILES):
                nc.vector.tensor_tensor(
                    out=dev[:, t, cols], in0=mu_q[:, t, cols], in1=mup_sb[:, t, cols], op=ALU.subtract
                )
            for t in range(B_TILES):
                nc.vector.tensor_tensor(
                    out=dev[:, t, cols], in0=dev[:, t, cols], in1=inv_std_p[:, t, cols], op=ALU.mult
                )
                nc.scalar.activation(
                    out=dev_sq[:, t, cols_of(part)],
                    in_=dev[:, t, cols_of(part)],
                    func=ACT.Square,
                    accum_out=kl_sum(DEV_SQ, part, t),
                )

        (lv0, lv1), (mu0, mu1) = W2_ORDER[:Z_PARTS], W2_ORDER[Z_PARTS:]
        group_w2([(lv0, 0), (lv0, 1)], "SS")
        group_w2([(lv0, 2), (lv1, 0)], "SS")
        layer1(10)
        layer1(11)
        quantise_waiting()
        quantise_hid(PASSES2 - 1)
        group_w2([(lv1, 1), (lv1, 2)], "SS")
        quantise_waiting()
        group_w2([(mu0, 0), (mu0, 1)], "SS")
        nc.scalar.activation(out=inv_std_p[:], in_=lvp_sb[:], func=ACT.Exp, scale=-0.5)
        lv_accs = [layer2(lv0)]
        group_w2([(mu0, 2), (mu1, 0)], "SS")
        add_bias(lv_q, lv_accs[0], lv0, 0)
        lv_accs.append(layer2(lv1))
        quantise_waiting()
        group_w2([(mu1, 1), (mu1, 2)], "SS")
        add_bias(lv_q, lv_accs[1], lv1, 1)
        clip_and_std(0)
        mu_accs = [layer2(mu0)]
        quantise_waiting()
        clip_and_std(1)
        diff_banks = [lv_diff_bank(0)]
        add_bias(mu_q, mu_accs[0], mu0, 0)
        store(out_1, mu_q, 0)
        mu_accs.append(layer2(mu1))
        diff_banks.append(lv_diff_bank(1))
        sum_var_ratio(0, diff_banks[0])
        combine(z_sb, std_q, eps_sb, ALU.mult, 0)
        sum_dev_squares(0)
        add_bias(mu_q, mu_accs[1], mu1, 1)
        store(out_1, mu_q, 1)
        sum_var_ratio(1, diff_banks[1])
        combine(z_sb, std_q, eps_sb, ALU.mult, 1)
        sum_dev_squares(1)
        combine(z_sb, z_sb, mu_q, ALU.add, 0)
        store(out_0, z_sb, 0)
        combine(z_sb, z_sb, mu_q, ALU.add, 1)
        store(out_0, z_sb, 1)

        kl_bank = psum_t.tile([P, 4 * P], F32, tag="bank")
        kl_order = [term * Z_PARTS + part for term in (LV_DIFF, VAR_RATIO, DEV_SQ) for part in range(Z_PARTS)]
        for j in kl_order:
            nc.tensor.matmul(
                out=kl_bank[:, 0:P],
                lhsT=kl_sums[:, j, :],
                rhs=ident[:],
                start=(j == kl_order[0]),
                stop=(j == kl_order[-1]),
            )
        kl_rows = keep.tile([P, P], F32)
        nc.scalar.activation(out=kl_rows[:], in_=kl_bank[:, 0:P], func=ACT.Copy, scale=0.5, bias=-0.5 * Z)
        nc.scalar.dma_start(out=out_3.rearrange("(t p) -> t p", p=P), in_=kl_rows[0:B_TILES, :])
